import numpy as np
import ml_dtypes


def mxq(x, axis, fmt="e4m3"):
    dtype, down = {"e4m3": (ml_dtypes.float8_e4m3fn, 7), "e5m2": (ml_dtypes.float8_e5m2, 14)}[fmt]
    v = np.moveaxis(np.asarray(x, np.float32).astype(ml_dtypes.bfloat16).astype(np.float64), axis, -1)
    blocks = v.reshape(v.shape[:-1] + (-1, 32))
    amax = np.abs(blocks).max(-1, keepdims=True)
    byte = np.maximum(np.where(amax > 0, np.frexp(amax)[1] - 1 + 127, 0) - down, 1)
    scale = np.exp2(byte - 127.0)
    codes = (blocks / scale).astype(np.float32).astype(dtype).astype(np.float64)
    return np.moveaxis((codes * scale).reshape(v.shape), -1, axis)


WIDE = False


def mx_kscale(k):
    if not WIDE:
        return np.ones(k)
    levels = np.array([10, -10, 5, -5, 0])
    a = np.random.permutation(np.resize(levels, k // 512 * 4)).reshape(k // 512, 4)
    idx = np.arange(k)
    return np.exp2(a[idx // 512, idx % 128 // 32])


BF16 = ml_dtypes.bfloat16


def bf(x):
    return np.asarray(x, np.float32).astype(BF16)


def f64(x):
    return np.asarray(x).astype(np.float64)


E2M1 = np.array([0.0, 0.5, 1.0, 1.5, 2.0, 3.0, 4.0, 6.0, -0.0, -0.5, -1.0, -1.5, -2.0, -3.0, -4.0, -6.0])


def pack_weight(w, fmt):
    k, n = w.shape
    w = f64(bf(w)).reshape(k // 32, 32, n)
    amax = np.abs(w).max(1)
    if fmt == "e4m3":
        byte = np.frexp(amax)[1] - 1 + 127 - 7
    else:
        mant, ex = np.frexp(amax / 6.0)
        byte = np.where(mant > 0.5, ex, ex - 1) + 127
    byte = np.clip(np.where(amax > 0, byte, 1), 1, 254)
    scaled = (w * np.exp2(127.0 - byte)[:, None, :]).reshape(k, n).astype(np.float32)
    by_word = np.ascontiguousarray(scaled.reshape(k // 512, 128, 4, n).transpose(0, 1, 3, 2))
    if fmt == "e4m3":
        words = by_word.astype(ml_dtypes.float8_e4m3fn).view(np.uint8)
    else:
        c = by_word.astype(ml_dtypes.float4_e2m1fn).view(np.uint8) & 0xF
        words = c[..., 0::2] | (c[..., 1::2] << 4)
    return np.ascontiguousarray(words), np.ascontiguousarray(byte.astype(np.uint8).reshape(k // 512, 16, n))


def unpack_weight(words, scales, fmt):
    g, p, n, _ = words.shape
    if fmt == "e4m3":
        vals = np.ascontiguousarray(words).view(ml_dtypes.float8_e4m3fn).astype(np.float64)
    else:
        nib = np.empty((g, p, n, 4), np.uint8)
        nib[..., 0::2] = words & 0xF
        nib[..., 1::2] = words >> 4
        vals = E2M1[nib]
    vals = vals * np.repeat(np.exp2(scales.astype(np.float64) - 127.0), 8, axis=1)[..., None]
    return vals.transpose(0, 1, 3, 2).reshape(g * 512, n)

def pack4(w):
    words, scales = pack_weight(w, "e2m1")
    return words.reshape(words.shape[0], 128, -1), scales


def unpack4(words, scales):
    return unpack_weight(words.reshape(words.shape[0], 128, -1, 2), scales, "e2m1")


B, N, C, F = 8, 32, 1024, 256
EPS_STD = 1e-5


def setup_inputs():
    u, s = mx_kscale(C), mx_kscale(C)
    rows = np.concatenate([u, u, s])
    x = bf(np.random.standard_normal((B, N, C)) * u)
    e_enc = bf(np.random.standard_normal((B, N, N, C)) * s)
    words, scales = pack4(np.random.standard_normal((3 * C, F)) / np.sqrt(3 * C) / rows[:, None])
    b_pre = bf(np.random.standard_normal(F) * 0.3)
    return {"x": x,
            "e_enc": e_enc,
            "W_pre_words": words,
            "W_pre_scales": scales,
            "b_pre": b_pre}


def reference(x, e_enc, W_pre_words, W_pre_scales, b_pre):
    w = unpack4(W_pre_words, W_pre_scales)
    xq = mxq(f64(x), 2, "e4m3")
    tgt = xq @ w[:C]
    src = xq @ w[C:2 * C]
    edg = mxq(f64(e_enc), 3, "e4m3") @ w[2 * C:]
    m = tgt[:, :, None, :] + src[:, None, :, :] + edg + f64(b_pre)
    mean = m.mean(axis=2)
    mn = m.min(axis=2)
    mx = m.max(axis=2)
    var = (m * m).mean(axis=2) - mean * mean
    std = np.sqrt(np.maximum(var, 0.0) + EPS_STD)
    return np.concatenate([mean, mn, mx, std], axis=-1)

@@ -1,0 +1,250 @@
+from contextlib import ExitStack
+
+import concourse.mybir as mybir
+from concourse.masks import make_identity
+
+F32 = mybir.dt.float32
+BF16 = mybir.dt.bfloat16
+I32 = mybir.dt.int32
+U32 = mybir.dt.uint32
+U8 = mybir.dt.uint8
+FP8X4 = mybir.dt.float8_e4m3fn_x4
+FP4X4 = mybir.dt.float4_e2m1fn_x4
+ALU = mybir.AluOpType
+ACT = mybir.ActivationFunctionType
+AXIS_X = mybir.AxisListType.X
+
+B, N, C, F = 8, 32, 1024, 256
+EPS_STD = 1e-5
+P = 128
+K_PASS = 4 * P
+PASSES = C // K_PASS
+W_TGT, W_SRC, W_EDGE = 0, PASSES, 2 * PASSES
+F_HALVES = F // P
+B_TILE = P // N
+B_HALVES = B // B_TILE
+I_ROUND = 2
+TILES = I_ROUND * B_HALVES
+COLS = TILES * P
+PAIRS = I_ROUND * B
+ROUNDS = N // I_ROUND
+AHEAD = 3
+
+FLOPS = 2 * (B * N * N + 2 * B * N) * C * F
+
+
+def tile_gnnlayer_pa_t_kernel(tc, x, e_enc, W_pre_words, W_pre_scales, b_pre, out):
+    nc = tc.nc
+    with ExitStack() as stack:
+        keep = stack.enter_context(tc.tile_pool(name="keep", bufs=1))
+        rows_pool = stack.enter_context(tc.tile_pool(name="rows", bufs=AHEAD * TILES))
+        stage = stack.enter_context(tc.tile_pool(name="stage", bufs=2))
+        turned_pool = stack.enter_context(tc.psum_pool(name="turned", bufs=4))
+        acc_pool = stack.enter_context(tc.psum_pool(name="acc", bufs=4))
+        stack.enter_context(tc.manual_schedule())
+
+        w_scales = keep.tile([P, 3 * PASSES, F], U8, align_bytes=64)
+        nc.vector.memset(w_scales[:].bitcast(I32), 0)
+        for quadrant in range(4):
+            nc.sync.dma_start(
+                out=w_scales[32 * quadrant : 32 * quadrant + 4].bitcast(I32),
+                in_=W_pre_scales.bitcast(I32)[:, 4 * quadrant : 4 * quadrant + 4, :].rearrange(
+                    "g s n -> s g n"
+                ),
+            )
+
+        def load_rows(source):
+            rows = rows_pool.tile([P, C], BF16)
+            nc.sync.dma_start(out=rows[:], in_=source.rearrange("b j k -> j b k"))
+            return rows
+
+        def graphs(half):
+            return slice(B_TILE * half, B_TILE * (half + 1))
+
+        x_rows = [load_rows(x[graphs(half)]) for half in range(B_HALVES)]
+
+        w_words = keep.tile([P, 3 * PASSES, 2 * F], U8, align_bytes=64)
+        nc.sync.dma_start(
+            out=w_words[:].bitcast(I32), in_=W_pre_words.bitcast(I32).rearrange("g p n -> p g n")
+        )
+        bias_rows = keep.tile([P, P], BF16)
+        nc.vector.memset(bias_rows[:], 0.0)
+        nc.sync.dma_start(
+            out=bias_rows[0:F_HALVES, :], in_=b_pre.rearrange("(h f) -> h f", h=F_HALVES)
+        )
+
+        def load_round(r):
+            return [
+                load_rows(e_enc[graphs(half), I_ROUND * r + i])
+                for i in range(I_ROUND)
+                for half in range(B_HALVES)
+            ]
+
+        e_rows = {r: load_round(r) for r in range(AHEAD)}
+
+        one = keep.tile([P, 1], F32)
+        nc.vector.memset(one[:], 1.0)
+        nc.scalar.activation(out=one[:], in_=one[:], func=ACT.Sqrt)
+
+        ident = keep.tile([P, P], F32)
+        make_identity(nc, ident[:])
+        perm = keep.tile([P, P], F32)
+        nc.vector.tensor_copy(
+            out=perm[:].rearrange("p (b j) -> p b j", b=B_TILE),
+            in_=ident[:].rearrange("p (j b) -> p b j", b=B_TILE),
+        )
+
+        def turn_rows(rows, grouped, first_col):
+            words = rows[:].bitcast(F32)
+            turned = turned_pool.tile([P, PASSES, 2, P], F32)
+            for g in range(PASSES):
+                for u in range(2):
+                    nc.tensor.transpose(
+                        turned[:, g, u, :], words[:, 2 * P * g + u : 2 * P * (g + 1) : 2], perm[:]
+                    )
+            nc.scalar.copy(
+                out=grouped[:, :, first_col : first_col + P, :],
+                in_=turned[:].rearrange("p g u r -> p g r u"),
+            )
+
+        def weight(g, h):
+            return {
+                "lhsT": w_words[:, g, 2 * P * h : 2 * P * (h + 1)].bitcast(FP4X4),
+                "lhsT_scale": w_scales[:, g, P * h : P * (h + 1)],
+            }
+
+        x_grouped = keep.tile([P, PASSES, B * N, 2], F32, align_bytes=64)
+        for half in range(B_HALVES):
+            turn_rows(x_rows[half], x_grouped, P * half)
+        x_codes = keep.tile([P, PASSES, I_ROUND, B * N], U32, align_bytes=64)
+        x_scales = keep.tile([P, PASSES, I_ROUND, B * N], U8, align_bytes=64)
+        for g in range(PASSES):
+            for i in range(I_ROUND):
+                nc.vector.quantize_mx(
+                    out=x_codes[:, g, i, :].bitcast(FP8X4),
+                    scales=x_scales[:, g, i, :],
+                    in_=x_grouped[:, g].rearrange("p c u -> p (c u)").bitcast(BF16),
+                )
+
+        def x_operand(g):
+            return {
+                "rhs": x_codes[:, g].rearrange("p i c -> p (i c)").bitcast(FP8X4),
+                "rhs_scale": x_scales[:, g].rearrange("p i c -> p (i c)"),
+            }
+
+        bias_rows32 = keep.tile([P, P], F32)
+        nc.vector.tensor_copy(out=bias_rows32[:], in_=bias_rows[:])
+        bias_turned = turned_pool.tile([P, PASSES, 2, P], F32, tag="turned")
+        nc.tensor.transpose(bias_turned[:, 0, 0, :], bias_rows32[:], ident[:])
+        bias = keep.tile([P, F_HALVES], F32)
+        nc.vector.tensor_copy(out=bias[:], in_=bias_turned[:, 0, 0, 0:F_HALVES])
+
+        def quantise_round(r):
+            grouped = stage.tile([P, PASSES, COLS, 2], F32, align_bytes=64)
+            for t in range(TILES):
+                turn_rows(e_rows[r][t], grouped, P * t)
+            codes = stage.tile([P, PASSES, COLS], U32, align_bytes=64)
+            scales = stage.tile([P, PASSES, COLS], U8, align_bytes=64)
+            nc.vector.quantize_mx(
+                out=codes[:].rearrange("p g c -> p (g c)").bitcast(FP8X4),
+                scales=scales[:].rearrange("p g c -> p (g c)"),
+                in_=grouped[:].rearrange("p g c u -> p (g c u)").bitcast(BF16),
+            )
+            return codes, scales
+
+        quantised = {0: quantise_round(0)}
+
+        tgt_bias = keep.tile([P, F_HALVES, N, B], F32)
+        for h in range(F_HALVES):
+            acc = acc_pool.tile([P, COLS], F32)
+            for g in range(PASSES):
+                nc.tensor.matmul_mx(
+                    out=acc[:], start=(g == 0), stop=(g == PASSES - 1),
+                    **weight(W_TGT + g, h), **x_operand(g),
+                )
+            nc.scalar.activation(
+                out=tgt_bias[:, h],
+                in_=acc[:, 0 : B * N].rearrange("p (b i) -> p i b", b=B),
+                func=ACT.Identity,
+                bias=bias[:, h : h + 1],
+            )
+
+        sums = keep.tile([P, F_HALVES, N * B], F32)
+        mins = keep.tile([P, F_HALVES, N * B], F32)
+        maxs = keep.tile([P, F_HALVES, N * B], F32)
+        square_sums = keep.tile([P, F_HALVES, N * B], F32)
+
+        def aggregate_round(r):
+            codes, scales = quantised[r]
+            pairs = slice(PAIRS * r, PAIRS * (r + 1))
+            squares = stage.tile([P, F_HALVES, PAIRS, N], F32)
+            for h in range(F_HALVES):
+                acc = acc_pool.tile([P, COLS], F32)
+                for g in range(PASSES):
+                    nc.tensor.matmul_mx(
+                        out=acc[:], start=(g == 0), stop=False, **weight(W_EDGE + g, h),
+                        rhs=codes[:, g, :].bitcast(FP8X4), rhs_scale=scales[:, g, :],
+                    )
+                for g in range(PASSES):
+                    nc.tensor.matmul_mx(
+                        out=acc[:], start=False, stop=(g == PASSES - 1),
+                        **weight(W_SRC + g, h), **x_operand(g),
+                    )
+                by_pair = acc[:].rearrange("p (c j) -> p c j", j=N)
+                nc.scalar.activation(out=squares[:, h], in_=by_pair, func=ACT.Square)
+                nc.vector.tensor_reduce(out=sums[:, h, pairs], in_=by_pair, axis=AXIS_X, op=ALU.add)
+                nc.vector.tensor_reduce(out=mins[:, h, pairs], in_=by_pair, axis=AXIS_X, op=ALU.min)
+                nc.vector.tensor_reduce(out=maxs[:, h, pairs], in_=by_pair, axis=AXIS_X, op=ALU.max)
+            width = N // 2
+            while width > 1:
+                nc.gpsimd.tensor_tensor(
+                    out=squares[:, :, :, 0:width], in0=squares[:, :, :, 0:width],
+                    in1=squares[:, :, :, width : 2 * width], op=ALU.add,
+                )
+                width //= 2
+            nc.gpsimd.tensor_tensor(
+                out=square_sums[:, :, pairs], in0=squares[:, :, :, 0], in1=squares[:, :, :, 1],
+                op=ALU.add,
+            )
+
+        for r in range(ROUNDS):
+            if r + AHEAD < ROUNDS:
+                e_rows[r + AHEAD] = load_round(r + AHEAD)
+            if r + 1 < ROUNDS:
+                quantised[r + 1] = quantise_round(r + 1)
+            aggregate_round(r)
+
+        flat_tgt_bias = tgt_bias[:].rearrange("p h i b -> p h (i b)")
+        result = keep.tile([P, 4, F_HALVES, N * B], F32)
+        mean_s = keep.tile([P, F_HALVES, N * B], F32)
+        nc.vector.tensor_scalar_mul(out=mean_s[:], in0=sums[:], scalar1=1.0 / N)
+        nc.vector.tensor_tensor(out=result[:, 0], in0=mean_s[:], in1=flat_tgt_bias, op=ALU.add)
+        nc.vector.tensor_tensor(out=result[:, 1], in0=mins[:], in1=flat_tgt_bias, op=ALU.add)
+        nc.vector.tensor_tensor(out=result[:, 2], in0=maxs[:], in1=flat_tgt_bias, op=ALU.add)
+        var = keep.tile([P, F_HALVES, N * B], F32)
+        nc.vector.tensor_tensor(out=var[:], in0=mean_s[:], in1=mean_s[:], op=ALU.mult)
+        nc.vector.scalar_tensor_tensor(
+            out=var[:], in0=square_sums[:], scalar=1.0 / N, in1=var[:],
+            op0=ALU.mult, op1=ALU.subtract,
+        )
+        nc.vector.tensor_scalar(
+            out=var[:], in0=var[:], scalar1=0.0, scalar2=EPS_STD, op0=ALU.max, op1=ALU.add
+        )
+        nc.scalar.activation(out=result[:, 3], in_=var[:], func=ACT.Sqrt)
+
+        out_by_i = out.rearrange("b i c -> i b c")
+        i_tile = P // B
+        for t in range(N // i_tile):
+            out_rows = stage.tile([P, 4 * F], F32)
+            for pair in range(2):
+                back = turned_pool.tile([P, 2, F_HALVES, P], F32, tag="turned")
+                for a in range(2):
+                    for h in range(F_HALVES):
+                        nc.tensor.transpose(
+                            back[:, a, h, :], result[:, 2 * pair + a, h, P * t : P * (t + 1)], ident[:]
+                        )
+                nc.scalar.copy(
+                    out=out_rows[:, 2 * F * pair : 2 * F * (pair + 1)],
+                    in_=back[:].rearrange("p a h f -> p (a h f)"),
+                )
+            nc.sync.dma_start(out=out_by_i[i_tile * t : i_tile * (t + 1)], in_=out_rows[:])

@@ -28,7 +28,11 @@ TILES = I_ROUND * B_HALVES
 COLS = TILES * P
 PAIRS = I_ROUND * B
 ROUNDS = N // I_ROUND
-AHEAD = 3
+I_STORE = P // B
+ROUNDS_STORE = I_STORE // I_ROUND
+LOAD_AHEAD = 4
+TARGET_ROUND = 2
+FINISH_LAG = 3
 
 FLOPS = 2 * (B * N * N + 2 * B * N) * C * F
 
@@ -37,11 +41,27 @@ def tile_gnnlayer_pa_t_kernel(tc, x, e_enc, W_pre_words, W_pre_scales, b_pre, ou
     nc = tc.nc
     with ExitStack() as stack:
         keep = stack.enter_context(tc.tile_pool(name="keep", bufs=1))
-        rows_pool = stack.enter_context(tc.tile_pool(name="rows", bufs=AHEAD * TILES))
+        rows_pool = stack.enter_context(tc.tile_pool(name="rows", bufs=LOAD_AHEAD * TILES))
         stage = stack.enter_context(tc.tile_pool(name="stage", bufs=2))
+        squares_pool = stack.enter_context(tc.tile_pool(name="squares", bufs=4))
         turned_pool = stack.enter_context(tc.psum_pool(name="turned", bufs=4))
         acc_pool = stack.enter_context(tc.psum_pool(name="acc", bufs=4))
         stack.enter_context(tc.manual_schedule())
+
+        def graphs(half):
+            return slice(B_TILE * half, B_TILE * (half + 1))
+
+        def load_rows(rows, source):
+            nc.sync.dma_start(out=rows[:], in_=source.rearrange("b j k -> j b k"))
+
+        def load_round(r):
+            tiles = []
+            for i in range(I_ROUND):
+                for half in range(B_HALVES):
+                    e_tile = rows_pool.tile([P, C], BF16)
+                    load_rows(e_tile, e_enc[graphs(half), I_ROUND * r + i])
+                    tiles.append(e_tile)
+            return tiles
 
         w_scales = keep.tile([P, 3 * PASSES, F], U8, align_bytes=64)
         nc.vector.memset(w_scales[:].bitcast(I32), 0)
@@ -52,35 +72,21 @@ def tile_gnnlayer_pa_t_kernel(tc, x, e_enc, W_pre_words, W_pre_scales, b_pre, ou
                     "g s n -> s g n"
                 ),
             )
-
-        def load_rows(source):
-            rows = rows_pool.tile([P, C], BF16)
-            nc.sync.dma_start(out=rows[:], in_=source.rearrange("b j k -> j b k"))
-            return rows
-
-        def graphs(half):
-            return slice(B_TILE * half, B_TILE * (half + 1))
-
-        x_rows = [load_rows(x[graphs(half)]) for half in range(B_HALVES)]
-
+        x_rows = keep.tile([P, B_HALVES, C], BF16)
+        for half in range(B_HALVES):
+            load_rows(x_rows[:, half, :], x[graphs(half)])
         w_words = keep.tile([P, 3 * PASSES, 2 * F], U8, align_bytes=64)
         nc.sync.dma_start(
             out=w_words[:].bitcast(I32), in_=W_pre_words.bitcast(I32).rearrange("g p n -> p g n")
         )
+        e_rows = {0: load_round(0)}
         bias_rows = keep.tile([P, P], BF16)
         nc.vector.memset(bias_rows[:], 0.0)
         nc.sync.dma_start(
             out=bias_rows[0:F_HALVES, :], in_=b_pre.rearrange("(h f) -> h f", h=F_HALVES)
         )
-
-        def load_round(r):
-            return [
-                load_rows(e_enc[graphs(half), I_ROUND * r + i])
-                for i in range(I_ROUND)
-                for half in range(B_HALVES)
-            ]
-
-        e_rows = {r: load_round(r) for r in range(AHEAD)}
+        for r in range(1, LOAD_AHEAD):
+            e_rows[r] = load_round(r)
 
         one = keep.tile([P, 1], F32)
         nc.vector.memset(one[:], 1.0)
@@ -95,7 +101,7 @@ def tile_gnnlayer_pa_t_kernel(tc, x, e_enc, W_pre_words, W_pre_scales, b_pre, ou
         )
 
         def turn_rows(rows, grouped, first_col):
-            words = rows[:].bitcast(F32)
+            words = rows.bitcast(F32)
             turned = turned_pool.tile([P, PASSES, 2, P], F32)
             for g in range(PASSES):
                 for u in range(2):
@@ -115,7 +121,7 @@ def tile_gnnlayer_pa_t_kernel(tc, x, e_enc, W_pre_words, W_pre_scales, b_pre, ou
 
         x_grouped = keep.tile([P, PASSES, B * N, 2], F32, align_bytes=64)
         for half in range(B_HALVES):
-            turn_rows(x_rows[half], x_grouped, P * half)
+            turn_rows(x_rows[:, half, :], x_grouped, P * half)
         x_codes = keep.tile([P, PASSES, I_ROUND, B * N], U32, align_bytes=64)
         x_scales = keep.tile([P, PASSES, I_ROUND, B * N], U8, align_bytes=64)
         for g in range(PASSES):
@@ -132,42 +138,24 @@ def tile_gnnlayer_pa_t_kernel(tc, x, e_enc, W_pre_words, W_pre_scales, b_pre, ou
                 "rhs_scale": x_scales[:, g].rearrange("p i c -> p (i c)"),
             }
 
-        bias_rows32 = keep.tile([P, P], F32)
-        nc.vector.tensor_copy(out=bias_rows32[:], in_=bias_rows[:])
-        bias_turned = turned_pool.tile([P, PASSES, 2, P], F32, tag="turned")
-        nc.tensor.transpose(bias_turned[:, 0, 0, :], bias_rows32[:], ident[:])
-        bias = keep.tile([P, F_HALVES], F32)
-        nc.vector.tensor_copy(out=bias[:], in_=bias_turned[:, 0, 0, 0:F_HALVES])
+        grouped_of = {}
+        quantised = {}
 
-        def quantise_round(r):
+        def turn_round(r):
             grouped = stage.tile([P, PASSES, COLS, 2], F32, align_bytes=64)
             for t in range(TILES):
-                turn_rows(e_rows[r][t], grouped, P * t)
+                turn_rows(e_rows[r][t][:], grouped, P * t)
+            grouped_of[r] = grouped
+
+        def quantise_round(r):
             codes = stage.tile([P, PASSES, COLS], U32, align_bytes=64)
             scales = stage.tile([P, PASSES, COLS], U8, align_bytes=64)
             nc.vector.quantize_mx(
                 out=codes[:].rearrange("p g c -> p (g c)").bitcast(FP8X4),
                 scales=scales[:].rearrange("p g c -> p (g c)"),
-                in_=grouped[:].rearrange("p g c u -> p (g c u)").bitcast(BF16),
+                in_=grouped_of[r][:].rearrange("p g c u -> p (g c u)").bitcast(BF16),
             )
-            return codes, scales
-
-        quantised = {0: quantise_round(0)}
-
-        tgt_bias = keep.tile([P, F_HALVES, N, B], F32)
-        for h in range(F_HALVES):
-            acc = acc_pool.tile([P, COLS], F32)
-            for g in range(PASSES):
-                nc.tensor.matmul_mx(
-                    out=acc[:], start=(g == 0), stop=(g == PASSES - 1),
-                    **weight(W_TGT + g, h), **x_operand(g),
-                )
-            nc.scalar.activation(
-                out=tgt_bias[:, h],
-                in_=acc[:, 0 : B * N].rearrange("p (b i) -> p i b", b=B),
-                func=ACT.Identity,
-                bias=bias[:, h : h + 1],
-            )
+            quantised[r] = (codes, scales)
 
         sums = keep.tile([P, F_HALVES, N * B], F32)
         mins = keep.tile([P, F_HALVES, N * B], F32)
@@ -177,7 +165,7 @@ def tile_gnnlayer_pa_t_kernel(tc, x, e_enc, W_pre_words, W_pre_scales, b_pre, ou
         def aggregate_round(r):
             codes, scales = quantised[r]
             pairs = slice(PAIRS * r, PAIRS * (r + 1))
-            squares = stage.tile([P, F_HALVES, PAIRS, N], F32)
+            squares = squares_pool.tile([P, F_HALVES, PAIRS, N], F32)
             for h in range(F_HALVES):
                 acc = acc_pool.tile([P, COLS], F32)
                 for g in range(PASSES):
@@ -207,44 +195,92 @@ def tile_gnnlayer_pa_t_kernel(tc, x, e_enc, W_pre_words, W_pre_scales, b_pre, ou
                 op=ALU.add,
             )
 
-        for r in range(ROUNDS):
-            if r + AHEAD < ROUNDS:
-                e_rows[r + AHEAD] = load_round(r + AHEAD)
-            if r + 1 < ROUNDS:
-                quantised[r + 1] = quantise_round(r + 1)
-            aggregate_round(r)
-
-        flat_tgt_bias = tgt_bias[:].rearrange("p h i b -> p h (i b)")
+        tgt_bias = keep.tile([P, F_HALVES, N * B], F32)
         result = keep.tile([P, 4, F_HALVES, N * B], F32)
         mean_s = keep.tile([P, F_HALVES, N * B], F32)
-        nc.vector.tensor_scalar_mul(out=mean_s[:], in0=sums[:], scalar1=1.0 / N)
-        nc.vector.tensor_tensor(out=result[:, 0], in0=mean_s[:], in1=flat_tgt_bias, op=ALU.add)
-        nc.vector.tensor_tensor(out=result[:, 1], in0=mins[:], in1=flat_tgt_bias, op=ALU.add)
-        nc.vector.tensor_tensor(out=result[:, 2], in0=maxs[:], in1=flat_tgt_bias, op=ALU.add)
-        var = keep.tile([P, F_HALVES, N * B], F32)
-        nc.vector.tensor_tensor(out=var[:], in0=mean_s[:], in1=mean_s[:], op=ALU.mult)
-        nc.vector.scalar_tensor_tensor(
-            out=var[:], in0=square_sums[:], scalar=1.0 / N, in1=var[:],
-            op0=ALU.mult, op1=ALU.subtract,
-        )
-        nc.vector.tensor_scalar(
-            out=var[:], in0=var[:], scalar1=0.0, scalar2=EPS_STD, op0=ALU.max, op1=ALU.add
-        )
-        nc.scalar.activation(out=result[:, 3], in_=var[:], func=ACT.Sqrt)
+        var_n = keep.tile([P, F_HALVES, N * B], F32)
+
+        def finish(store, engine):
+            cols = slice(P * store, P * (store + 1))
+            engine.tensor_scalar(
+                out=mean_s[:, :, cols], in0=sums[:, :, cols],
+                scalar1=1.0 / N, scalar2=0.0, op0=ALU.mult, op1=ALU.add,
+            )
+            for a, aggregate in enumerate((mean_s, mins, maxs)):
+                engine.tensor_tensor(
+                    out=result[:, a, :, cols], in0=aggregate[:, :, cols], in1=tgt_bias[:, :, cols],
+                    op=ALU.add,
+                )
+            engine.tensor_tensor(
+                out=var_n[:, :, cols], in0=mean_s[:, :, cols], in1=sums[:, :, cols], op=ALU.mult
+            )
+            engine.tensor_tensor(
+                out=var_n[:, :, cols], in0=square_sums[:, :, cols], in1=var_n[:, :, cols],
+                op=ALU.subtract,
+            )
+            engine.tensor_scalar(
+                out=var_n[:, :, cols], in0=var_n[:, :, cols],
+                scalar1=0.0, scalar2=0.0, op0=ALU.max, op1=ALU.add,
+            )
 
         out_by_i = out.rearrange("b i c -> i b c")
-        i_tile = P // B
-        for t in range(N // i_tile):
+
+        def store_rows(store):
+            cols = slice(P * store, P * (store + 1))
+            nc.scalar.activation(
+                out=result[:, 3, :, cols], in_=var_n[:, :, cols], func=ACT.Sqrt,
+                scale=1.0 / N, bias=eps[:],
+            )
             out_rows = stage.tile([P, 4 * F], F32)
             for pair in range(2):
                 back = turned_pool.tile([P, 2, F_HALVES, P], F32, tag="turned")
                 for a in range(2):
                     for h in range(F_HALVES):
-                        nc.tensor.transpose(
-                            back[:, a, h, :], result[:, 2 * pair + a, h, P * t : P * (t + 1)], ident[:]
-                        )
-                nc.scalar.copy(
-                    out=out_rows[:, 2 * F * pair : 2 * F * (pair + 1)],
-                    in_=back[:].rearrange("p a h f -> p (a h f)"),
+                        nc.tensor.transpose(back[:, a, h, :], result[:, 2 * pair + a, h, cols], ident[:])
+                half_row = slice(2 * F * pair, 2 * F * (pair + 1))
+                nc.scalar.copy(out=out_rows[:, half_row], in_=back[:].rearrange("p a h f -> p (a h f)"))
+                nc.sync.dma_start(
+                    out=out_by_i[I_STORE * store : I_STORE * (store + 1), :, half_row],
+                    in_=out_rows[:, half_row],
                 )
-            nc.sync.dma_start(out=out_by_i[i_tile * t : i_tile * (t + 1)], in_=out_rows[:])
+
+        eps = keep.tile([P, 1], F32)
+        nc.vector.memset(eps[:], EPS_STD)
+
+        def target_term():
+            bias_rows32 = keep.tile([P, P], F32)
+            nc.vector.tensor_copy(out=bias_rows32[:], in_=bias_rows[:])
+            bias_turned = turned_pool.tile([P, PASSES, 2, P], F32, tag="turned")
+            nc.tensor.transpose(bias_turned[:, 0, 0, :], bias_rows32[:], ident[:])
+            bias = keep.tile([P, F_HALVES], F32)
+            nc.vector.tensor_copy(out=bias[:], in_=bias_turned[:, 0, 0, 0:F_HALVES])
+            for h in range(F_HALVES):
+                acc = acc_pool.tile([P, COLS], F32)
+                for g in range(PASSES):
+                    nc.tensor.matmul_mx(
+                        out=acc[:], start=(g == 0), stop=(g == PASSES - 1),
+                        **weight(W_TGT + g, h), **x_operand(g),
+                    )
+                nc.scalar.activation(
+                    out=tgt_bias[:, h].rearrange("p (i b) -> p i b", b=B),
+                    in_=acc[:, 0 : B * N].rearrange("p (b i) -> p i b", b=B),
+                    func=ACT.Identity,
+                    bias=bias[:, h : h + 1],
+                )
+
+        turn_round(0)
+        quantise_round(0)
+        for r in range(ROUNDS):
+            if r + LOAD_AHEAD < ROUNDS:
+                e_rows[r + LOAD_AHEAD] = load_round(r + LOAD_AHEAD)
+            if r + 1 < ROUNDS:
+                turn_round(r + 1)
+                quantise_round(r + 1)
+            if r == TARGET_ROUND:
+                target_term()
+            aggregate_round(r)
+            if r == ROUNDS_STORE - 1 + FINISH_LAG:
+                finish(0, nc.gpsimd)
+        store_rows(0)
+        finish(1, nc.vector)
+        store_rows(1)

@@ -33,6 +33,7 @@ ROUNDS_STORE = I_STORE // I_ROUND
 LOAD_AHEAD = 4
 TARGET_ROUND = 2
 FINISH_LAG = 3
+HALVINGS = 2
 
 FLOPS = 2 * (B * N * N + 2 * B * N) * C * F
 
@@ -161,6 +162,7 @@ def tile_gnnlayer_pa_t_kernel(tc, x, e_enc, W_pre_words, W_pre_scales, b_pre, ou
         mins = keep.tile([P, F_HALVES, N * B], F32)
         maxs = keep.tile([P, F_HALVES, N * B], F32)
         square_sums = keep.tile([P, F_HALVES, N * B], F32)
+        squares_of = {}
 
         def aggregate_round(r):
             codes, scales = quantised[r]
@@ -183,16 +185,18 @@ def tile_gnnlayer_pa_t_kernel(tc, x, e_enc, W_pre_words, W_pre_scales, b_pre, ou
                 nc.vector.tensor_reduce(out=sums[:, h, pairs], in_=by_pair, axis=AXIS_X, op=ALU.add)
                 nc.vector.tensor_reduce(out=mins[:, h, pairs], in_=by_pair, axis=AXIS_X, op=ALU.min)
                 nc.vector.tensor_reduce(out=maxs[:, h, pairs], in_=by_pair, axis=AXIS_X, op=ALU.max)
-            width = N // 2
-            while width > 1:
+            for halving in range(1, HALVINGS + 1):
+                width = N >> halving
                 nc.gpsimd.tensor_tensor(
                     out=squares[:, :, :, 0:width], in0=squares[:, :, :, 0:width],
                     in1=squares[:, :, :, width : 2 * width], op=ALU.add,
                 )
-                width //= 2
-            nc.gpsimd.tensor_tensor(
-                out=square_sums[:, :, pairs], in0=squares[:, :, :, 0], in1=squares[:, :, :, 1],
-                op=ALU.add,
+            squares_of[r] = squares
+
+        def sum_squares(r):
+            nc.vector.tensor_reduce(
+                out=square_sums[:, :, PAIRS * r : PAIRS * (r + 1)],
+                in_=squares_of[r][:, :, :, 0 : N >> HALVINGS], axis=AXIS_X, op=ALU.add,
             )
 
         tgt_bias = keep.tile([P, F_HALVES, N * B], F32)
@@ -279,8 +283,11 @@ def tile_gnnlayer_pa_t_kernel(tc, x, e_enc, W_pre_words, W_pre_scales, b_pre, ou
             if r == TARGET_ROUND:
                 target_term()
             aggregate_round(r)
+            if r > 0:
+                sum_squares(r - 1)
             if r == ROUNDS_STORE - 1 + FINISH_LAG:
                 finish(0, nc.gpsimd)
         store_rows(0)
+        sum_squares(ROUNDS - 1)
         finish(1, nc.vector)
         store_rows(1)

@@ -163,6 +163,7 @@ def tile_gnnlayer_pa_t_kernel(tc, x, e_enc, W_pre_words, W_pre_scales, b_pre, ou
         maxs = keep.tile([P, F_HALVES, N * B], F32)
         square_sums = keep.tile([P, F_HALVES, N * B], F32)
         squares_of = {}
+        waited = keep.tile([P, 1], U32)
 
         def aggregate_round(r):
             codes, scales = quantised[r]
@@ -185,6 +186,8 @@ def tile_gnnlayer_pa_t_kernel(tc, x, e_enc, W_pre_words, W_pre_scales, b_pre, ou
                 nc.vector.tensor_reduce(out=sums[:, h, pairs], in_=by_pair, axis=AXIS_X, op=ALU.add)
                 nc.vector.tensor_reduce(out=mins[:, h, pairs], in_=by_pair, axis=AXIS_X, op=ALU.min)
                 nc.vector.tensor_reduce(out=maxs[:, h, pairs], in_=by_pair, axis=AXIS_X, op=ALU.max)
+            if r + 1 in quantised:
+                nc.gpsimd.tensor_copy(out=waited[:], in_=quantised[r + 1][0][:, 0, 0:1])
             for halving in range(1, HALVINGS + 1):
                 width = N >> halving
                 nc.gpsimd.tensor_tensor(

@@ -32,8 +32,8 @@ I_STORE = P // B
 ROUNDS_STORE = I_STORE // I_ROUND
 LOAD_AHEAD = 4
 TARGET_ROUND = 2
-FINISH_LAG = 3
-HALVINGS = 2
+LEFT = N // 4
+FINISH_FROM = ROUNDS_STORE + 1
 
 FLOPS = 2 * (B * N * N + 2 * B * N) * C * F
 
@@ -161,8 +161,10 @@ def tile_gnnlayer_pa_t_kernel(tc, x, e_enc, W_pre_words, W_pre_scales, b_pre, ou
         sums = keep.tile([P, F_HALVES, N * B], F32)
         mins = keep.tile([P, F_HALVES, N * B], F32)
         maxs = keep.tile([P, F_HALVES, N * B], F32)
-        square_sums = keep.tile([P, F_HALVES, N * B], F32)
-        squares_of = {}
+        partial = keep.tile([P, F_HALVES, N * B, LEFT], F32)
+        partial_last = keep.tile([P, F_HALVES, PAIRS, LEFT], F32)
+        last_pairs = slice(PAIRS * (ROUNDS - 1), PAIRS * ROUNDS)
+        nc.gpsimd.memset(partial[:, :, last_pairs, :], 0.0)
         waited = keep.tile([P, 1], U32)
 
         def aggregate_round(r):
@@ -188,71 +190,81 @@ def tile_gnnlayer_pa_t_kernel(tc, x, e_enc, W_pre_words, W_pre_scales, b_pre, ou
                 nc.vector.tensor_reduce(out=maxs[:, h, pairs], in_=by_pair, axis=AXIS_X, op=ALU.max)
             if r + 1 in quantised:
                 nc.gpsimd.tensor_copy(out=waited[:], in_=quantised[r + 1][0][:, 0, 0:1])
-            for halving in range(1, HALVINGS + 1):
-                width = N >> halving
-                nc.gpsimd.tensor_tensor(
-                    out=squares[:, :, :, 0:width], in0=squares[:, :, :, 0:width],
-                    in1=squares[:, :, :, width : 2 * width], op=ALU.add,
-                )
-            squares_of[r] = squares
-
-        def sum_squares(r):
-            nc.vector.tensor_reduce(
-                out=square_sums[:, :, PAIRS * r : PAIRS * (r + 1)],
-                in_=squares_of[r][:, :, :, 0 : N >> HALVINGS], axis=AXIS_X, op=ALU.add,
+            nc.gpsimd.tensor_tensor(
+                out=squares[:, :, :, 0 : 2 * LEFT], in0=squares[:, :, :, 0 : 2 * LEFT],
+                in1=squares[:, :, :, 2 * LEFT : 4 * LEFT], op=ALU.add,
+            )
+            nc.gpsimd.tensor_tensor(
+                out=partial_last[:] if r == ROUNDS - 1 else partial[:, :, pairs, :],
+                in0=squares[:, :, :, 0:LEFT], in1=squares[:, :, :, LEFT : 2 * LEFT], op=ALU.add,
             )
 
         tgt_bias = keep.tile([P, F_HALVES, N * B], F32)
-        result = keep.tile([P, 4, F_HALVES, N * B], F32)
-        mean_s = keep.tile([P, F_HALVES, N * B], F32)
-        var_n = keep.tile([P, F_HALVES, N * B], F32)
-
-        def finish(store, engine):
-            cols = slice(P * store, P * (store + 1))
-            engine.tensor_scalar(
-                out=mean_s[:, :, cols], in0=sums[:, :, cols],
-                scalar1=1.0 / N, scalar2=0.0, op0=ALU.mult, op1=ALU.add,
-            )
-            for a, aggregate in enumerate((mean_s, mins, maxs)):
-                engine.tensor_tensor(
-                    out=result[:, a, :, cols], in0=aggregate[:, :, cols], in1=tgt_bias[:, :, cols],
-                    op=ALU.add,
-                )
-            engine.tensor_tensor(
-                out=var_n[:, :, cols], in0=mean_s[:, :, cols], in1=sums[:, :, cols], op=ALU.mult
-            )
-            engine.tensor_tensor(
-                out=var_n[:, :, cols], in0=square_sums[:, :, cols], in1=var_n[:, :, cols],
-                op=ALU.subtract,
-            )
-            engine.tensor_scalar(
-                out=var_n[:, :, cols], in0=var_n[:, :, cols],
-                scalar1=0.0, scalar2=0.0, op0=ALU.max, op1=ALU.add,
-            )
-
+        tgt_bias_n = keep.tile([P, F_HALVES, N * B], F32)
+        minus_square = keep.tile([P, F_HALVES, N * B], F32)
         out_by_i = out.rearrange("b i c -> i b c")
-
-        def store_rows(store):
-            cols = slice(P * store, P * (store + 1))
-            nc.scalar.activation(
-                out=result[:, 3, :, cols], in_=var_n[:, :, cols], func=ACT.Sqrt,
-                scale=1.0 / N, bias=eps[:],
-            )
-            out_rows = stage.tile([P, 4 * F], F32)
-            for pair in range(2):
-                back = turned_pool.tile([P, 2, F_HALVES, P], F32, tag="turned")
-                for a in range(2):
-                    for h in range(F_HALVES):
-                        nc.tensor.transpose(back[:, a, h, :], result[:, 2 * pair + a, h, cols], ident[:])
-                half_row = slice(2 * F * pair, 2 * F * (pair + 1))
-                nc.scalar.copy(out=out_rows[:, half_row], in_=back[:].rearrange("p a h f -> p (a h f)"))
-                nc.sync.dma_start(
-                    out=out_by_i[I_STORE * store : I_STORE * (store + 1), :, half_row],
-                    in_=out_rows[:, half_row],
-                )
-
+        out_rows_of = {}
         eps = keep.tile([P, 1], F32)
         nc.vector.memset(eps[:], EPS_STD)
+
+        def targets(store):
+            return slice(P * store, P * (store + 1))
+
+        def turn_and_add(back, terms, opens=True, closes=True):
+            for t, term in enumerate(terms):
+                nc.tensor.matmul(
+                    out=back, lhsT=term, rhs=ident[:], is_transpose=True,
+                    start=(opens and t == 0), stop=(closes and t == len(terms) - 1),
+                )
+
+        def store_columns(store, first, width):
+            nc.sync.dma_start(
+                out=out_by_i[I_STORE * store : I_STORE * (store + 1), :, first : first + width],
+                in_=out_rows_of[store][:, first : first + width],
+            )
+
+        def square_the_sums(store):
+            cols = targets(store)
+            nc.vector.scalar_tensor_tensor(
+                out=minus_square[:, :, cols], in0=sums[:, :, cols], scalar=-1.0 / N,
+                in1=sums[:, :, cols], op0=ALU.mult, op1=ALU.mult,
+            )
+
+        def finish_extremes(store, copy):
+            cols = targets(store)
+            out_rows = stage.tile([P, 4 * F], F32)
+            out_rows_of[store] = out_rows
+            back = turned_pool.tile([P, 2, F_HALVES, P], F32, tag="turned")
+            for a, aggregate in enumerate((mins, maxs)):
+                for h in range(F_HALVES):
+                    turn_and_add(back[:, a, h, :], [aggregate[:, h, cols], tgt_bias[:, h, cols]])
+            copy(out=out_rows[:, F : 3 * F], in_=back[:].rearrange("p a h f -> p (a h f)"))
+
+        def finish_mean(store):
+            cols = targets(store)
+            back = turned_pool.tile([P, F_HALVES, P], F32, tag="turned")
+            for h in range(F_HALVES):
+                turn_and_add(back[:, h, :], [sums[:, h, cols], tgt_bias_n[:, h, cols]])
+            nc.scalar.activation(
+                out=out_rows_of[store][:, 0:F], in_=back[:].rearrange("p h f -> p (h f)"),
+                func=ACT.Copy, scale=1.0 / N,
+            )
+
+        def open_std(store, h):
+            back = turned_pool.tile([P, P], F32, tag="turned")
+            turn_and_add(
+                back[:], [partial[:, h, targets(store), t] for t in range(LEFT)], closes=False
+            )
+            return back
+
+        def close_std(store, h, back):
+            turn_and_add(back[:], [minus_square[:, h, targets(store)]], opens=False)
+            variance = stage.tile([P, P], F32)
+            nc.scalar.activation(out=variance[:], in_=back[:], func=ACT.Relu, scale=1.0 / N)
+            nc.scalar.activation(
+                out=out_rows_of[store][:, 3 * F + P * h : 3 * F + P * (h + 1)], in_=variance[:],
+                func=ACT.Sqrt, bias=eps[:],
+            )
 
         def target_term():
             bias_rows32 = keep.tile([P, P], F32)
@@ -274,6 +286,10 @@ def tile_gnnlayer_pa_t_kernel(tc, x, e_enc, W_pre_words, W_pre_scales, b_pre, ou
                     func=ACT.Identity,
                     bias=bias[:, h : h + 1],
                 )
+            nc.gpsimd.tensor_scalar(
+                out=tgt_bias_n[:], in0=tgt_bias[:], scalar1=float(N), scalar2=0.0,
+                op0=ALU.mult, op1=ALU.add,
+            )
 
         turn_round(0)
         quantise_round(0)
@@ -285,12 +301,29 @@ def tile_gnnlayer_pa_t_kernel(tc, x, e_enc, W_pre_words, W_pre_scales, b_pre, ou
                 quantise_round(r + 1)
             if r == TARGET_ROUND:
                 target_term()
+            if r == FINISH_FROM:
+                square_the_sums(0)
+                finish_extremes(0, nc.scalar.copy)
+            elif r == FINISH_FROM + 1:
+                finish_mean(0)
+            elif r == FINISH_FROM + 2:
+                close_std(0, 0, open_std(0, 0))
+            elif r == FINISH_FROM + 3:
+                close_std(0, 1, open_std(0, 1))
+                store_columns(0, 0, 4 * F)
             aggregate_round(r)
-            if r > 0:
-                sum_squares(r - 1)
-            if r == ROUNDS_STORE - 1 + FINISH_LAG:
-                finish(0, nc.gpsimd)
-        store_rows(0)
-        sum_squares(ROUNDS - 1)
-        finish(1, nc.vector)
-        store_rows(1)
+        open_groups = [open_std(1, h) for h in range(F_HALVES)]
+        last_squares = keep.tile([P, F_HALVES, PAIRS], F32)
+        nc.vector.tensor_reduce(out=last_squares[:], in_=partial_last[:], axis=AXIS_X, op=ALU.add)
+        square_the_sums(1)
+        nc.vector.tensor_tensor(
+            out=minus_square[:, :, last_pairs], in0=minus_square[:, :, last_pairs],
+            in1=last_squares[:], op=ALU.add,
+        )
+        finish_extremes(1, nc.vector.tensor_copy)
+        store_columns(1, F, 2 * F)
+        for h in range(F_HALVES):
+            close_std(1, h, open_groups[h])
+        store_columns(1, 3 * F, F)
+        finish_mean(1)
+        store_columns(1, 0, F)

@@ -64,6 +64,10 @@ def tile_gnnlayer_pa_t_kernel(tc, x, e_enc, W_pre_words, W_pre_scales, b_pre, ou
                     tiles.append(e_tile)
             return tiles
 
+        x_rows = keep.tile([P, B_HALVES, C], BF16)
+        for half in range(B_HALVES):
+            load_rows(x_rows[:, half, :], x[graphs(half)])
+        e_rows = {0: load_round(0)}
         w_scales = keep.tile([P, 3 * PASSES, F], U8, align_bytes=64)
         nc.vector.memset(w_scales[:].bitcast(I32), 0)
         for quadrant in range(4):
@@ -73,14 +77,10 @@ def tile_gnnlayer_pa_t_kernel(tc, x, e_enc, W_pre_words, W_pre_scales, b_pre, ou
                     "g s n -> s g n"
                 ),
             )
-        x_rows = keep.tile([P, B_HALVES, C], BF16)
-        for half in range(B_HALVES):
-            load_rows(x_rows[:, half, :], x[graphs(half)])
         w_words = keep.tile([P, 3 * PASSES, 2 * F], U8, align_bytes=64)
         nc.sync.dma_start(
             out=w_words[:].bitcast(I32), in_=W_pre_words.bitcast(I32).rearrange("g p n -> p g n")
         )
-        e_rows = {0: load_round(0)}
         bias_rows = keep.tile([P, P], BF16)
         nc.vector.memset(bias_rows[:], 0.0)
         nc.sync.dma_start(
@@ -230,7 +230,7 @@ def tile_gnnlayer_pa_t_kernel(tc, x, e_enc, W_pre_words, W_pre_scales, b_pre, ou
                 in1=sums[:, :, cols], op0=ALU.mult, op1=ALU.mult,
             )
 
-        def finish_extremes(store, copy):
+        def finish_extremes(store):
             cols = targets(store)
             out_rows = stage.tile([P, 4 * F], F32)
             out_rows_of[store] = out_rows
@@ -238,7 +238,7 @@ def tile_gnnlayer_pa_t_kernel(tc, x, e_enc, W_pre_words, W_pre_scales, b_pre, ou
             for a, aggregate in enumerate((mins, maxs)):
                 for h in range(F_HALVES):
                     turn_and_add(back[:, a, h, :], [aggregate[:, h, cols], tgt_bias[:, h, cols]])
-            copy(out=out_rows[:, F : 3 * F], in_=back[:].rearrange("p a h f -> p (a h f)"))
+            nc.scalar.copy(out=out_rows[:, F : 3 * F], in_=back[:].rearrange("p a h f -> p (a h f)"))
 
         def finish_mean(store):
             cols = targets(store)
@@ -250,6 +250,39 @@ def tile_gnnlayer_pa_t_kernel(tc, x, e_enc, W_pre_words, W_pre_scales, b_pre, ou
                 func=ACT.Copy, scale=1.0 / N,
             )
 
+        tgt_bias_rows = keep.tile([P, F], F32)
+
+        def turn_target_term(store):
+            back = turned_pool.tile([P, F_HALVES, P], F32, tag="turned")
+            for h in range(F_HALVES):
+                turn_and_add(back[:, h, :], [tgt_bias[:, h, targets(store)]])
+            nc.scalar.copy(out=tgt_bias_rows[:], in_=back[:].rearrange("p h f -> p (h f)"))
+
+        def finish_extremes_at_the_end(store):
+            cols = targets(store)
+            out_rows = stage.tile([P, 4 * F], F32)
+            out_rows_of[store] = out_rows
+            back = turned_pool.tile([P, 2, F_HALVES, P], F32, tag="turned")
+            for a, aggregate in enumerate((mins, maxs)):
+                for h in range(F_HALVES):
+                    turn_and_add(back[:, a, h, :], [aggregate[:, h, cols]])
+            for a in range(2):
+                nc.vector.tensor_tensor(
+                    out=out_rows[:, F * (a + 1) : F * (a + 2)],
+                    in0=back[:, a].rearrange("p h f -> p (h f)"), in1=tgt_bias_rows[:], op=ALU.add,
+                )
+
+        def finish_mean_at_the_end(store):
+            back = turned_pool.tile([P, F_HALVES, P], F32, tag="turned")
+            for h in range(F_HALVES):
+                turn_and_add(back[:, h, :], [sums[:, h, targets(store)]])
+            nc.vector.scalar_tensor_tensor(
+                out=out_rows_of[store][:, 0:F], in0=back[:].rearrange("p h f -> p (h f)"),
+                scalar=1.0 / N, in1=tgt_bias_rows[:], op0=ALU.mult, op1=ALU.add,
+            )
+
+        variance = keep.tile([P, F], F32)
+
         def open_std(store, h):
             back = turned_pool.tile([P, P], F32, tag="turned")
             turn_and_add(
@@ -259,12 +292,14 @@ def tile_gnnlayer_pa_t_kernel(tc, x, e_enc, W_pre_words, W_pre_scales, b_pre, ou
 
         def close_std(store, h, back):
             turn_and_add(back[:], [minus_square[:, h, targets(store)]], opens=False)
-            variance = stage.tile([P, P], F32)
-            nc.scalar.activation(out=variance[:], in_=back[:], func=ACT.Relu, scale=1.0 / N)
             nc.scalar.activation(
-                out=out_rows_of[store][:, 3 * F + P * h : 3 * F + P * (h + 1)], in_=variance[:],
-                func=ACT.Sqrt, bias=eps[:],
+                out=variance[:, P * h : P * (h + 1)], in_=back[:], func=ACT.Relu, scale=1.0 / N
             )
+            if h == F_HALVES - 1:
+                nc.scalar.activation(
+                    out=out_rows_of[store][:, 3 * F : 4 * F], in_=variance[:], func=ACT.Sqrt,
+                    bias=eps[:],
+                )
 
         def target_term():
             bias_rows32 = keep.tile([P, P], F32)
@@ -303,7 +338,7 @@ def tile_gnnlayer_pa_t_kernel(tc, x, e_enc, W_pre_words, W_pre_scales, b_pre, ou
                 target_term()
             if r == FINISH_FROM:
                 square_the_sums(0)
-                finish_extremes(0, nc.scalar.copy)
+                finish_extremes(0)
             elif r == FINISH_FROM + 1:
                 finish_mean(0)
             elif r == FINISH_FROM + 2:
@@ -311,6 +346,8 @@ def tile_gnnlayer_pa_t_kernel(tc, x, e_enc, W_pre_words, W_pre_scales, b_pre, ou
             elif r == FINISH_FROM + 3:
                 close_std(0, 1, open_std(0, 1))
                 store_columns(0, 0, 4 * F)
+            elif r == FINISH_FROM + 4:
+                turn_target_term(1)
             aggregate_round(r)
         open_groups = [open_std(1, h) for h in range(F_HALVES)]
         last_squares = keep.tile([P, F_HALVES, PAIRS], F32)
@@ -320,10 +357,10 @@ def tile_gnnlayer_pa_t_kernel(tc, x, e_enc, W_pre_words, W_pre_scales, b_pre, ou
             out=minus_square[:, :, last_pairs], in0=minus_square[:, :, last_pairs],
             in1=last_squares[:], op=ALU.add,
         )
-        finish_extremes(1, nc.vector.tensor_copy)
+        finish_extremes_at_the_end(1)
         store_columns(1, F, 2 * F)
         for h in range(F_HALVES):
             close_std(1, h, open_groups[h])
         store_columns(1, 3 * F, F)
-        finish_mean(1)
+        finish_mean_at_the_end(1)
         store_columns(1, 0, F)

@@ -338,17 +338,13 @@ def tile_gnnlayer_pa_t_kernel(tc, x, e_enc, W_pre_words, W_pre_scales, b_pre, ou
                 target_term()
             if r == FINISH_FROM:
                 square_the_sums(0)
-                finish_extremes(0)
-            elif r == FINISH_FROM + 1:
-                finish_mean(0)
-            elif r == FINISH_FROM + 2:
-                close_std(0, 0, open_std(0, 0))
-            elif r == FINISH_FROM + 3:
-                close_std(0, 1, open_std(0, 1))
-                store_columns(0, 0, 4 * F)
-            elif r == FINISH_FROM + 4:
-                turn_target_term(1)
             aggregate_round(r)
+        finish_extremes(0)
+        finish_mean(0)
+        for h in range(F_HALVES):
+            close_std(0, h, open_std(0, h))
+        store_columns(0, 0, 4 * F)
+        turn_target_term(1)
         open_groups = [open_std(1, h) for h in range(F_HALVES)]
         last_squares = keep.tile([P, F_HALVES, PAIRS], F32)
         nc.vector.tensor_reduce(out=last_squares[:], in_=partial_last[:], axis=AXIS_X, op=ALU.add)

@@ -165,7 +165,6 @@ def tile_gnnlayer_pa_t_kernel(tc, x, e_enc, W_pre_words, W_pre_scales, b_pre, ou
         partial_last = keep.tile([P, F_HALVES, PAIRS, LEFT], F32)
         last_pairs = slice(PAIRS * (ROUNDS - 1), PAIRS * ROUNDS)
         nc.gpsimd.memset(partial[:, :, last_pairs, :], 0.0)
-        waited = keep.tile([P, 1], U32)
 
         def aggregate_round(r):
             codes, scales = quantised[r]
@@ -188,8 +187,6 @@ def tile_gnnlayer_pa_t_kernel(tc, x, e_enc, W_pre_words, W_pre_scales, b_pre, ou
                 nc.vector.tensor_reduce(out=sums[:, h, pairs], in_=by_pair, axis=AXIS_X, op=ALU.add)
                 nc.vector.tensor_reduce(out=mins[:, h, pairs], in_=by_pair, axis=AXIS_X, op=ALU.min)
                 nc.vector.tensor_reduce(out=maxs[:, h, pairs], in_=by_pair, axis=AXIS_X, op=ALU.max)
-            if r + 1 in quantised:
-                nc.gpsimd.tensor_copy(out=waited[:], in_=quantised[r + 1][0][:, 0, 0:1])
             nc.gpsimd.tensor_tensor(
                 out=squares[:, :, :, 0 : 2 * LEFT], in0=squares[:, :, :, 0 : 2 * LEFT],
                 in1=squares[:, :, :, 2 * LEFT : 4 * LEFT], op=ALU.add,

@@ -1,4 +1,5 @@
 from contextlib import ExitStack
+from itertools import product
 
 import concourse.mybir as mybir
 from concourse.masks import make_identity
@@ -31,7 +32,6 @@ ROUNDS = N // I_ROUND
 I_STORE = P // B
 ROUNDS_STORE = I_STORE // I_ROUND
 LOAD_AHEAD = 4
-TARGET_ROUND = 2
 LEFT = N // 4
 FINISH_FROM = ROUNDS_STORE + 1
 
@@ -64,10 +64,10 @@ def tile_gnnlayer_pa_t_kernel(tc, x, e_enc, W_pre_words, W_pre_scales, b_pre, ou
                     tiles.append(e_tile)
             return tiles
 
+        e_rows = {0: load_round(0)}
         x_rows = keep.tile([P, B_HALVES, C], BF16)
         for half in range(B_HALVES):
             load_rows(x_rows[:, half, :], x[graphs(half)])
-        e_rows = {0: load_round(0)}
         w_scales = keep.tile([P, 3 * PASSES, F], U8, align_bytes=64)
         nc.vector.memset(w_scales[:].bitcast(I32), 0)
         for quadrant in range(4):
@@ -78,15 +78,22 @@ def tile_gnnlayer_pa_t_kernel(tc, x, e_enc, W_pre_words, W_pre_scales, b_pre, ou
                 ),
             )
         w_words = keep.tile([P, 3 * PASSES, 2 * F], U8, align_bytes=64)
-        nc.sync.dma_start(
-            out=w_words[:].bitcast(I32), in_=W_pre_words.bitcast(I32).rearrange("g p n -> p g n")
-        )
+
+        def load_words(first, end):
+            nc.sync.dma_start(
+                out=w_words[:, first:end].bitcast(I32),
+                in_=W_pre_words.bitcast(I32)[first:end].rearrange("g p n -> p g n"),
+            )
+
+        load_words(W_SRC, 3 * PASSES)
         bias_rows = keep.tile([P, P], BF16)
         nc.vector.memset(bias_rows[:], 0.0)
         nc.sync.dma_start(
             out=bias_rows[0:F_HALVES, :], in_=b_pre.rearrange("(h f) -> h f", h=F_HALVES)
         )
-        for r in range(1, LOAD_AHEAD):
+        e_rows[1] = load_round(1)
+        load_words(W_TGT, W_SRC)
+        for r in range(2, LOAD_AHEAD):
             e_rows[r] = load_round(r)
 
         one = keep.tile([P, 1], F32)
@@ -101,7 +108,7 @@ def tile_gnnlayer_pa_t_kernel(tc, x, e_enc, W_pre_words, W_pre_scales, b_pre, ou
             in_=ident[:].rearrange("p (j b) -> p b j", b=B_TILE),
         )
 
-        def turn_rows(rows, grouped, first_col):
+        def turn_rows(rows, grouped, first_col, copy):
             words = rows.bitcast(F32)
             turned = turned_pool.tile([P, PASSES, 2, P], F32)
             for g in range(PASSES):
@@ -109,7 +116,7 @@ def tile_gnnlayer_pa_t_kernel(tc, x, e_enc, W_pre_words, W_pre_scales, b_pre, ou
                     nc.tensor.transpose(
                         turned[:, g, u, :], words[:, 2 * P * g + u : 2 * P * (g + 1) : 2], perm[:]
                     )
-            nc.scalar.copy(
+            copy(
                 out=grouped[:, :, first_col : first_col + P, :],
                 in_=turned[:].rearrange("p g u r -> p g r u"),
             )
@@ -121,17 +128,23 @@ def tile_gnnlayer_pa_t_kernel(tc, x, e_enc, W_pre_words, W_pre_scales, b_pre, ou
             }
 
         x_grouped = keep.tile([P, PASSES, B * N, 2], F32, align_bytes=64)
-        for half in range(B_HALVES):
-            turn_rows(x_rows[:, half, :], x_grouped, P * half)
         x_codes = keep.tile([P, PASSES, I_ROUND, B * N], U32, align_bytes=64)
         x_scales = keep.tile([P, PASSES, I_ROUND, B * N], U8, align_bytes=64)
-        for g in range(PASSES):
-            for i in range(I_ROUND):
-                nc.vector.quantize_mx(
-                    out=x_codes[:, g, i, :].bitcast(FP8X4),
-                    scales=x_scales[:, g, i, :],
-                    in_=x_grouped[:, g].rearrange("p c u -> p (c u)").bitcast(BF16),
-                )
+
+        copies = (nc.scalar.copy, nc.vector.tensor_copy)
+
+        def turn_x():
+            for half, copy in enumerate(copies):
+                turn_rows(x_rows[:, half, :], x_grouped, P * half, copy)
+
+        def quantise_x():
+            for g in range(PASSES):
+                for i in range(I_ROUND):
+                    nc.vector.quantize_mx(
+                        out=x_codes[:, g, i, :].bitcast(FP8X4),
+                        scales=x_scales[:, g, i, :],
+                        in_=x_grouped[:, g].rearrange("p c u -> p (c u)").bitcast(BF16),
+                    )
 
         def x_operand(g):
             return {
@@ -143,14 +156,31 @@ def tile_gnnlayer_pa_t_kernel(tc, x, e_enc, W_pre_words, W_pre_scales, b_pre, ou
         quantised = {}
 
         def turn_round(r):
-            grouped = stage.tile([P, PASSES, COLS, 2], F32, align_bytes=64)
+            grouped = stage.tile([P, PASSES, COLS, 2], F32, align_bytes=64, tag="grouped")
             for t in range(TILES):
-                turn_rows(e_rows[r][t][:], grouped, P * t)
+                turn_rows(e_rows[r][t][:], grouped, P * t, nc.scalar.copy)
             grouped_of[r] = grouped
 
+        def turn_and_quantise_first_round():
+            grouped = stage.tile([P, PASSES, COLS, 2], F32, align_bytes=64, tag="grouped")
+            codes = stage.tile([P, PASSES, COLS], U32, align_bytes=64, tag="codes")
+            scales = stage.tile([P, PASSES, COLS], U8, align_bytes=64, tag="scales")
+            for i in range(I_ROUND):
+                cols = slice(B * N * i, B * N * (i + 1))
+                for half, copy in enumerate(copies):
+                    t = B_HALVES * i + half
+                    turn_rows(e_rows[0][t][:], grouped, P * t, copy)
+                for g in range(PASSES):
+                    nc.vector.quantize_mx(
+                        out=codes[:, g, cols].bitcast(FP8X4),
+                        scales=scales[:, g, cols],
+                        in_=grouped[:, g, cols, :].rearrange("p c u -> p (c u)").bitcast(BF16),
+                    )
+            quantised[0] = (codes, scales)
+
         def quantise_round(r):
-            codes = stage.tile([P, PASSES, COLS], U32, align_bytes=64)
-            scales = stage.tile([P, PASSES, COLS], U8, align_bytes=64)
+            codes = stage.tile([P, PASSES, COLS], U32, align_bytes=64, tag="codes")
+            scales = stage.tile([P, PASSES, COLS], U8, align_bytes=64, tag="scales")
             nc.vector.quantize_mx(
                 out=codes[:].rearrange("p g c -> p (g c)").bitcast(FP8X4),
                 scales=scales[:].rearrange("p g c -> p (g c)"),
@@ -166,36 +196,66 @@ def tile_gnnlayer_pa_t_kernel(tc, x, e_enc, W_pre_words, W_pre_scales, b_pre, ou
         last_pairs = slice(PAIRS * (ROUNDS - 1), PAIRS * ROUNDS)
         nc.gpsimd.memset(partial[:, :, last_pairs, :], 0.0)
 
-        def aggregate_round(r):
-            codes, scales = quantised[r]
-            pairs = slice(PAIRS * r, PAIRS * (r + 1))
-            squares = squares_pool.tile([P, F_HALVES, PAIRS, N], F32)
+        accs_of = {}
+        squares_of = {}
+
+        def open_round(r):
+            accs = []
             for h in range(F_HALVES):
-                acc = acc_pool.tile([P, COLS], F32)
+                acc = acc_pool.tile([P, COLS], F32, tag="acc")
+                accs.append(acc)
+            accs_of[r] = accs
+            squares = squares_pool.tile([P, F_HALVES, PAIRS, N], F32)
+            squares_of[r] = squares
+
+        def add_edges(r, h, g):
+            codes, scales = quantised[r]
+            nc.tensor.matmul_mx(
+                out=accs_of[r][h][:], start=(g == 0), stop=False, **weight(W_EDGE + g, h),
+                rhs=codes[:, g, :].bitcast(FP8X4), rhs_scale=scales[:, g, :],
+            )
+
+        def add_sources(r, h, g):
+            nc.tensor.matmul_mx(
+                out=accs_of[r][h][:], start=False, stop=(g == PASSES - 1),
+                **weight(W_SRC + g, h), **x_operand(g),
+            )
+
+        def multiply(r, h):
+            for add in (add_edges, add_sources):
                 for g in range(PASSES):
-                    nc.tensor.matmul_mx(
-                        out=acc[:], start=(g == 0), stop=False, **weight(W_EDGE + g, h),
-                        rhs=codes[:, g, :].bitcast(FP8X4), rhs_scale=scales[:, g, :],
-                    )
-                for g in range(PASSES):
-                    nc.tensor.matmul_mx(
-                        out=acc[:], start=False, stop=(g == PASSES - 1),
-                        **weight(W_SRC + g, h), **x_operand(g),
-                    )
-                by_pair = acc[:].rearrange("p (c j) -> p c j", j=N)
-                nc.scalar.activation(out=squares[:, h], in_=by_pair, func=ACT.Square)
-                nc.vector.tensor_reduce(out=sums[:, h, pairs], in_=by_pair, axis=AXIS_X, op=ALU.add)
-                nc.vector.tensor_reduce(out=mins[:, h, pairs], in_=by_pair, axis=AXIS_X, op=ALU.min)
-                nc.vector.tensor_reduce(out=maxs[:, h, pairs], in_=by_pair, axis=AXIS_X, op=ALU.max)
+                    add(r, h, g)
+
+        def by_pair(r, h):
+            return accs_of[r][h][:].rearrange("p (c j) -> p c j", j=N)
+
+        def square(r, h):
+            nc.scalar.activation(out=squares_of[r][:, h], in_=by_pair(r, h), func=ACT.Square)
+
+        def reduce(r, h, aggregate, op):
+            nc.vector.tensor_reduce(
+                out=aggregate[:, h, PAIRS * r : PAIRS * (r + 1)], in_=by_pair(r, h),
+                axis=AXIS_X, op=op,
+            )
+
+        def reduce_all(r, h):
+            reduce(r, h, sums, ALU.add)
+            reduce(r, h, mins, ALU.min)
+            reduce(r, h, maxs, ALU.max)
+
+        def halve_squares(r):
+            squares = squares_of[r]
             nc.gpsimd.tensor_tensor(
                 out=squares[:, :, :, 0 : 2 * LEFT], in0=squares[:, :, :, 0 : 2 * LEFT],
                 in1=squares[:, :, :, 2 * LEFT : 4 * LEFT], op=ALU.add,
             )
+            pairs = slice(PAIRS * r, PAIRS * (r + 1))
             nc.gpsimd.tensor_tensor(
                 out=partial_last[:] if r == ROUNDS - 1 else partial[:, :, pairs, :],
                 in0=squares[:, :, :, 0:LEFT], in1=squares[:, :, :, LEFT : 2 * LEFT], op=ALU.add,
             )
 
+        bias = keep.tile([P, F_HALVES], F32)
         tgt_bias = keep.tile([P, F_HALVES, N * B], F32)
         tgt_bias_n = keep.tile([P, F_HALVES, N * B], F32)
         minus_square = keep.tile([P, F_HALVES, N * B], F32)
@@ -227,56 +287,42 @@ def tile_gnnlayer_pa_t_kernel(tc, x, e_enc, W_pre_words, W_pre_scales, b_pre, ou
                 in1=sums[:, :, cols], op0=ALU.mult, op1=ALU.mult,
             )
 
-        def finish_extremes(store):
-            cols = targets(store)
+        def open_rows(store):
             out_rows = stage.tile([P, 4 * F], F32)
             out_rows_of[store] = out_rows
-            back = turned_pool.tile([P, 2, F_HALVES, P], F32, tag="turned")
-            for a, aggregate in enumerate((mins, maxs)):
-                for h in range(F_HALVES):
-                    turn_and_add(back[:, a, h, :], [aggregate[:, h, cols], tgt_bias[:, h, cols]])
-            nc.scalar.copy(out=out_rows[:, F : 3 * F], in_=back[:].rearrange("p a h f -> p (a h f)"))
 
-        def finish_mean(store):
+        def finish_extreme(store, first, aggregate):
             cols = targets(store)
             back = turned_pool.tile([P, F_HALVES, P], F32, tag="turned")
             for h in range(F_HALVES):
-                turn_and_add(back[:, h, :], [sums[:, h, cols], tgt_bias_n[:, h, cols]])
+                turn_and_add(back[:, h, :], [tgt_bias[:, h, cols], aggregate[:, h, cols]])
+            nc.scalar.copy(
+                out=out_rows_of[store][:, first : first + F],
+                in_=back[:].rearrange("p h f -> p (h f)"),
+            )
+
+        def open_mean():
+            back = turned_pool.tile([P, F_HALVES, P], F32, tag="turned")
+            return back
+
+        def turn_mean(store, h, back):
+            cols = targets(store)
+            turn_and_add(back[:, h, :], [tgt_bias_n[:, h, cols], sums[:, h, cols]])
+
+        def copy_mean(store, back):
             nc.scalar.activation(
                 out=out_rows_of[store][:, 0:F], in_=back[:].rearrange("p h f -> p (h f)"),
                 func=ACT.Copy, scale=1.0 / N,
             )
 
-        tgt_bias_rows = keep.tile([P, F], F32)
-
-        def turn_target_term(store):
-            back = turned_pool.tile([P, F_HALVES, P], F32, tag="turned")
+        def finish_mean(store):
+            back = open_mean()
             for h in range(F_HALVES):
-                turn_and_add(back[:, h, :], [tgt_bias[:, h, targets(store)]])
-            nc.scalar.copy(out=tgt_bias_rows[:], in_=back[:].rearrange("p h f -> p (h f)"))
+                turn_mean(store, h, back)
+            copy_mean(store, back)
 
-        def finish_extremes_at_the_end(store):
-            cols = targets(store)
-            out_rows = stage.tile([P, 4 * F], F32)
-            out_rows_of[store] = out_rows
-            back = turned_pool.tile([P, 2, F_HALVES, P], F32, tag="turned")
-            for a, aggregate in enumerate((mins, maxs)):
-                for h in range(F_HALVES):
-                    turn_and_add(back[:, a, h, :], [aggregate[:, h, cols]])
-            for a in range(2):
-                nc.vector.tensor_tensor(
-                    out=out_rows[:, F * (a + 1) : F * (a + 2)],
-                    in0=back[:, a].rearrange("p h f -> p (h f)"), in1=tgt_bias_rows[:], op=ALU.add,
-                )
-
-        def finish_mean_at_the_end(store):
-            back = turned_pool.tile([P, F_HALVES, P], F32, tag="turned")
-            for h in range(F_HALVES):
-                turn_and_add(back[:, h, :], [sums[:, h, targets(store)]])
-            nc.vector.scalar_tensor_tensor(
-                out=out_rows_of[store][:, 0:F], in0=back[:].rearrange("p h f -> p (h f)"),
-                scalar=1.0 / N, in1=tgt_bias_rows[:], op0=ALU.mult, op1=ALU.add,
-            )
+        def finish_std(store, h):
+            close_std(store, h, open_std(store, h))
 
         variance = keep.tile([P, F], F32)
 
@@ -299,22 +345,23 @@ def tile_gnnlayer_pa_t_kernel(tc, x, e_enc, W_pre_words, W_pre_scales, b_pre, ou
                 )
 
         def target_term():
-            bias_rows32 = keep.tile([P, P], F32)
-            nc.vector.tensor_copy(out=bias_rows32[:], in_=bias_rows[:])
-            bias_turned = turned_pool.tile([P, PASSES, 2, P], F32, tag="turned")
-            nc.tensor.transpose(bias_turned[:, 0, 0, :], bias_rows32[:], ident[:])
-            bias = keep.tile([P, F_HALVES], F32)
-            nc.vector.tensor_copy(out=bias[:], in_=bias_turned[:, 0, 0, 0:F_HALVES])
+            acc = acc_pool.tile([P, F_HALVES, B * N], F32, tag="acc")
             for h in range(F_HALVES):
-                acc = acc_pool.tile([P, COLS], F32)
-                for g in range(PASSES):
-                    nc.tensor.matmul_mx(
-                        out=acc[:], start=(g == 0), stop=(g == PASSES - 1),
-                        **weight(W_TGT + g, h), **x_operand(g),
-                    )
+                for half in range(B_HALVES):
+                    cols = slice(P * half, P * (half + 1))
+                    for g in range(PASSES):
+                        nc.tensor.matmul_mx(
+                            out=acc[:, h, cols], start=(g == 0), stop=(g == PASSES - 1),
+                            **weight(W_TGT + g, h), rhs=x_codes[:, g, 0, cols].bitcast(FP8X4),
+                            rhs_scale=x_scales[:, g, 0, cols],
+                        )
+            return acc
+
+        def finish_target_term(acc):
+            for h in range(F_HALVES):
                 nc.scalar.activation(
                     out=tgt_bias[:, h].rearrange("p (i b) -> p i b", b=B),
-                    in_=acc[:, 0 : B * N].rearrange("p (b i) -> p i b", b=B),
+                    in_=acc[:, h].rearrange("p (b i) -> p i b", b=B),
                     func=ACT.Identity,
                     bias=bias[:, h : h + 1],
                 )
@@ -323,26 +370,66 @@ def tile_gnnlayer_pa_t_kernel(tc, x, e_enc, W_pre_words, W_pre_scales, b_pre, ou
                 op0=ALU.mult, op1=ALU.add,
             )
 
-        turn_round(0)
-        quantise_round(0)
-        for r in range(ROUNDS):
+        bias_rows32 = keep.tile([P, P], F32)
+
+        def turn_bias():
+            bias_turned = turned_pool.tile([P, P], F32, tag="turned")
+            nc.tensor.transpose(bias_turned[:], bias_rows32[:], ident[:])
+            nc.scalar.copy(out=bias[:], in_=bias_turned[:, 0:F_HALVES])
+
+        turn_and_quantise_first_round()
+        turn_x()
+        quantise_x()
+        nc.vector.tensor_copy(out=bias_rows32[:], in_=bias_rows[:])
+        open_round(0)
+        for add in (add_edges, add_sources):
+            for g, h in product(range(PASSES), range(F_HALVES)):
+                add(0, h, g)
+        reduce_all(0, 0)
+        square(0, 1)
+        reduce_all(0, 1)
+        e_rows[LOAD_AHEAD] = load_round(LOAD_AHEAD)
+        turn_round(1)
+        square(0, 0)
+        halve_squares(0)
+        quantise_round(1)
+        turn_bias()
+        target = target_term()
+        finish_steps = [
+            lambda: finish_extreme(0, F, mins),
+            lambda: finish_extreme(0, 2 * F, maxs),
+            lambda: finish_mean(0),
+            lambda: finish_std(0, 0),
+            lambda: finish_std(0, 1),
+            lambda: store_columns(0, 0, 4 * F),
+        ]
+        open_rows(0)
+        for r in range(1, ROUNDS):
             if r + LOAD_AHEAD < ROUNDS:
                 e_rows[r + LOAD_AHEAD] = load_round(r + LOAD_AHEAD)
             if r + 1 < ROUNDS:
                 turn_round(r + 1)
+            if r == 1:
+                finish_target_term(target)
+            if 0 <= r - FINISH_FROM < len(finish_steps):
+                finish_steps[r - FINISH_FROM]()
+            if r + 1 < ROUNDS:
                 quantise_round(r + 1)
-            if r == TARGET_ROUND:
-                target_term()
             if r == FINISH_FROM:
                 square_the_sums(0)
-            aggregate_round(r)
-        finish_extremes(0)
-        finish_mean(0)
-        for h in range(F_HALVES):
-            close_std(0, h, open_std(0, h))
-        store_columns(0, 0, 4 * F)
-        turn_target_term(1)
-        open_groups = [open_std(1, h) for h in range(F_HALVES)]
+            open_round(r)
+            for h in range(F_HALVES):
+                multiply(r, h)
+                square(r, h)
+                if r < ROUNDS - 1:
+                    reduce_all(r, h)
+            halve_squares(r)
+
+        last = ROUNDS - 1
+        reduce(last, 0, sums, ALU.add)
+        reduce(last, 0, mins, ALU.min)
+        reduce(last, 0, maxs, ALU.max)
+        reduce(last, 1, sums, ALU.add)
         last_squares = keep.tile([P, F_HALVES, PAIRS], F32)
         nc.vector.tensor_reduce(out=last_squares[:], in_=partial_last[:], axis=AXIS_X, op=ALU.add)
         square_the_sums(1)
@@ -350,10 +437,29 @@ def tile_gnnlayer_pa_t_kernel(tc, x, e_enc, W_pre_words, W_pre_scales, b_pre, ou
             out=minus_square[:, :, last_pairs], in0=minus_square[:, :, last_pairs],
             in1=last_squares[:], op=ALU.add,
         )
-        finish_extremes_at_the_end(1)
-        store_columns(1, F, 2 * F)
+        reduce(last, 1, mins, ALU.min)
+        reduce(last, 1, maxs, ALU.max)
+
+        open_rows(1)
+        cols = targets(1)
+        open_groups = [open_std(1, h) for h in range(F_HALVES)]
+        mean_back = open_mean()
+        turn_mean(1, 0, mean_back)
+        first_back = turned_pool.tile([P, 2, P], F32, tag="turned")
+        for a, aggregate in enumerate((mins, maxs)):
+            turn_and_add(first_back[:, a, :], [tgt_bias[:, 0, cols], aggregate[:, 0, cols]])
+        nc.scalar.copy(
+            out=out_rows_of[1][:, F : 3 * F].rearrange("p (a h f) -> p a h f", a=2, h=F_HALVES)[:, :, 0, :],
+            in_=first_back[:],
+        )
+        turn_mean(1, 1, mean_back)
+        copy_mean(1, mean_back)
+        store_columns(1, 0, F)
         for h in range(F_HALVES):
             close_std(1, h, open_groups[h])
         store_columns(1, 3 * F, F)
-        finish_mean_at_the_end(1)
-        store_columns(1, 0, F)
+        for first, aggregate in ((F, mins), (2 * F, maxs)):
+            back = turned_pool.tile([P, P], F32, tag="turned")
+            turn_and_add(back[:], [tgt_bias[:, 1, cols], aggregate[:, 1, cols]])
+            nc.scalar.copy(out=out_rows_of[1][:, first + P : first + F], in_=back[:])
+            store_columns(1, first, F)

@@ -32,7 +32,6 @@ ROUNDS = N // I_ROUND
 I_STORE = P // B
 ROUNDS_STORE = I_STORE // I_ROUND
 LOAD_AHEAD = 4
-LEFT = N // 4
 FINISH_FROM = ROUNDS_STORE + 1
 
 FLOPS = 2 * (B * N * N + 2 * B * N) * C * F
@@ -44,7 +43,6 @@ def tile_gnnlayer_pa_t_kernel(tc, x, e_enc, W_pre_words, W_pre_scales, b_pre, ou
         keep = stack.enter_context(tc.tile_pool(name="keep", bufs=1))
         rows_pool = stack.enter_context(tc.tile_pool(name="rows", bufs=LOAD_AHEAD * TILES))
         stage = stack.enter_context(tc.tile_pool(name="stage", bufs=2))
-        squares_pool = stack.enter_context(tc.tile_pool(name="squares", bufs=4))
         turned_pool = stack.enter_context(tc.psum_pool(name="turned", bufs=4))
         acc_pool = stack.enter_context(tc.psum_pool(name="acc", bufs=4))
         stack.enter_context(tc.manual_schedule())
@@ -188,16 +186,13 @@ def tile_gnnlayer_pa_t_kernel(tc, x, e_enc, W_pre_words, W_pre_scales, b_pre, ou
             )
             quantised[r] = (codes, scales)
 
-        sums = keep.tile([P, F_HALVES, N * B], F32)
+        stats = keep.tile([P, F_HALVES, N * B, 3], F32)
+        means = stats[:, :, :, 1]
+        variances_n = stats[:, :, :, 2]
         mins = keep.tile([P, F_HALVES, N * B], F32)
         maxs = keep.tile([P, F_HALVES, N * B], F32)
-        partial = keep.tile([P, F_HALVES, N * B, LEFT], F32)
-        partial_last = keep.tile([P, F_HALVES, PAIRS, LEFT], F32)
-        last_pairs = slice(PAIRS * (ROUNDS - 1), PAIRS * ROUNDS)
-        nc.gpsimd.memset(partial[:, :, last_pairs, :], 0.0)
 
         accs_of = {}
-        squares_of = {}
 
         def open_round(r):
             accs = []
@@ -205,8 +200,6 @@ def tile_gnnlayer_pa_t_kernel(tc, x, e_enc, W_pre_words, W_pre_scales, b_pre, ou
                 acc = acc_pool.tile([P, COLS], F32, tag="acc")
                 accs.append(acc)
             accs_of[r] = accs
-            squares = squares_pool.tile([P, F_HALVES, PAIRS, N], F32)
-            squares_of[r] = squares
 
         def add_edges(r, h, g):
             codes, scales = quantised[r]
@@ -226,39 +219,27 @@ def tile_gnnlayer_pa_t_kernel(tc, x, e_enc, W_pre_words, W_pre_scales, b_pre, ou
                 for g in range(PASSES):
                     add(r, h, g)
 
-        def by_pair(r, h):
-            return accs_of[r][h][:].rearrange("p (c j) -> p c j", j=N)
-
-        def square(r, h):
-            nc.scalar.activation(out=squares_of[r][:, h], in_=by_pair(r, h), func=ACT.Square)
-
         def reduce(r, h, aggregate, op):
             nc.vector.tensor_reduce(
-                out=aggregate[:, h, PAIRS * r : PAIRS * (r + 1)], in_=by_pair(r, h),
-                axis=AXIS_X, op=op,
+                out=aggregate[:, h, PAIRS * r : PAIRS * (r + 1)],
+                in_=accs_of[r][h][:].rearrange("p (c j) -> p c j", j=N), axis=AXIS_X, op=op,
             )
 
+        def mean_and_variance(r, h):
+            for c in range(0, PAIRS, 2):
+                pairs = slice(PAIRS * r + c, PAIRS * r + c + 2)
+                nc.vector.bn_stats(
+                    out=stats[:, h, pairs, :].rearrange("p c v -> p (c v)"),
+                    in_=accs_of[r][h][:, N * c : N * (c + 2)].rearrange("p (c j) -> p j c", c=2),
+                )
+
         def reduce_all(r, h):
-            reduce(r, h, sums, ALU.add)
+            mean_and_variance(r, h)
             reduce(r, h, mins, ALU.min)
             reduce(r, h, maxs, ALU.max)
 
-        def halve_squares(r):
-            squares = squares_of[r]
-            nc.gpsimd.tensor_tensor(
-                out=squares[:, :, :, 0 : 2 * LEFT], in0=squares[:, :, :, 0 : 2 * LEFT],
-                in1=squares[:, :, :, 2 * LEFT : 4 * LEFT], op=ALU.add,
-            )
-            pairs = slice(PAIRS * r, PAIRS * (r + 1))
-            nc.gpsimd.tensor_tensor(
-                out=partial_last[:] if r == ROUNDS - 1 else partial[:, :, pairs, :],
-                in0=squares[:, :, :, 0:LEFT], in1=squares[:, :, :, LEFT : 2 * LEFT], op=ALU.add,
-            )
-
         bias = keep.tile([P, F_HALVES], F32)
         tgt_bias = keep.tile([P, F_HALVES, N * B], F32)
-        tgt_bias_n = keep.tile([P, F_HALVES, N * B], F32)
-        minus_square = keep.tile([P, F_HALVES, N * B], F32)
         out_by_i = out.rearrange("b i c -> i b c")
         out_rows_of = {}
         eps = keep.tile([P, 1], F32)
@@ -267,11 +248,11 @@ def tile_gnnlayer_pa_t_kernel(tc, x, e_enc, W_pre_words, W_pre_scales, b_pre, ou
         def targets(store):
             return slice(P * store, P * (store + 1))
 
-        def turn_and_add(back, terms, opens=True, closes=True):
+        def turn_and_add(back, terms):
             for t, term in enumerate(terms):
                 nc.tensor.matmul(
                     out=back, lhsT=term, rhs=ident[:], is_transpose=True,
-                    start=(opens and t == 0), stop=(closes and t == len(terms) - 1),
+                    start=(t == 0), stop=(t == len(terms) - 1),
                 )
 
         def store_columns(store, first, width):
@@ -280,18 +261,11 @@ def tile_gnnlayer_pa_t_kernel(tc, x, e_enc, W_pre_words, W_pre_scales, b_pre, ou
                 in_=out_rows_of[store][:, first : first + width],
             )
 
-        def square_the_sums(store):
-            cols = targets(store)
-            nc.vector.scalar_tensor_tensor(
-                out=minus_square[:, :, cols], in0=sums[:, :, cols], scalar=-1.0 / N,
-                in1=sums[:, :, cols], op0=ALU.mult, op1=ALU.mult,
-            )
-
         def open_rows(store):
             out_rows = stage.tile([P, 4 * F], F32)
             out_rows_of[store] = out_rows
 
-        def finish_extreme(store, first, aggregate):
+        def finish(store, first, aggregate):
             cols = targets(store)
             back = turned_pool.tile([P, F_HALVES, P], F32, tag="turned")
             for h in range(F_HALVES):
@@ -301,48 +275,20 @@ def tile_gnnlayer_pa_t_kernel(tc, x, e_enc, W_pre_words, W_pre_scales, b_pre, ou
                 in_=back[:].rearrange("p h f -> p (h f)"),
             )
 
-        def open_mean():
-            back = turned_pool.tile([P, F_HALVES, P], F32, tag="turned")
-            return back
-
-        def turn_mean(store, h, back):
-            cols = targets(store)
-            turn_and_add(back[:, h, :], [tgt_bias_n[:, h, cols], sums[:, h, cols]])
-
-        def copy_mean(store, back):
-            nc.scalar.activation(
-                out=out_rows_of[store][:, 0:F], in_=back[:].rearrange("p h f -> p (h f)"),
-                func=ACT.Copy, scale=1.0 / N,
-            )
-
-        def finish_mean(store):
-            back = open_mean()
-            for h in range(F_HALVES):
-                turn_mean(store, h, back)
-            copy_mean(store, back)
-
-        def finish_std(store, h):
-            close_std(store, h, open_std(store, h))
-
         variance = keep.tile([P, F], F32)
 
-        def open_std(store, h):
-            back = turned_pool.tile([P, P], F32, tag="turned")
-            turn_and_add(
-                back[:], [partial[:, h, targets(store), t] for t in range(LEFT)], closes=False
-            )
-            return back
-
-        def close_std(store, h, back):
-            turn_and_add(back[:], [minus_square[:, h, targets(store)]], opens=False)
+        def finish_std(store):
+            back = turned_pool.tile([P, F_HALVES, P], F32, tag="turned")
+            for h in range(F_HALVES):
+                turn_and_add(back[:, h, :], [variances_n[:, h, targets(store)]])
             nc.scalar.activation(
-                out=variance[:, P * h : P * (h + 1)], in_=back[:], func=ACT.Relu, scale=1.0 / N
+                out=variance[:], in_=back[:].rearrange("p h f -> p (h f)"), func=ACT.Relu,
+                scale=1.0 / N,
             )
-            if h == F_HALVES - 1:
-                nc.scalar.activation(
-                    out=out_rows_of[store][:, 3 * F : 4 * F], in_=variance[:], func=ACT.Sqrt,
-                    bias=eps[:],
-                )
+            nc.scalar.activation(
+                out=out_rows_of[store][:, 3 * F : 4 * F], in_=variance[:], func=ACT.Sqrt,
+                bias=eps[:],
+            )
 
         def target_term():
             acc = acc_pool.tile([P, F_HALVES, B * N], F32, tag="acc")
@@ -365,10 +311,6 @@ def tile_gnnlayer_pa_t_kernel(tc, x, e_enc, W_pre_words, W_pre_scales, b_pre, ou
                     func=ACT.Identity,
                     bias=bias[:, h : h + 1],
                 )
-            nc.gpsimd.tensor_scalar(
-                out=tgt_bias_n[:], in0=tgt_bias[:], scalar1=float(N), scalar2=0.0,
-                op0=ALU.mult, op1=ALU.add,
-            )
 
         bias_rows32 = keep.tile([P, P], F32)
 
@@ -385,22 +327,18 @@ def tile_gnnlayer_pa_t_kernel(tc, x, e_enc, W_pre_words, W_pre_scales, b_pre, ou
         for add in (add_edges, add_sources):
             for g, h in product(range(PASSES), range(F_HALVES)):
                 add(0, h, g)
-        reduce_all(0, 0)
-        square(0, 1)
-        reduce_all(0, 1)
+        for h in range(F_HALVES):
+            reduce_all(0, h)
         e_rows[LOAD_AHEAD] = load_round(LOAD_AHEAD)
         turn_round(1)
-        square(0, 0)
-        halve_squares(0)
         quantise_round(1)
         turn_bias()
         target = target_term()
         finish_steps = [
-            lambda: finish_extreme(0, F, mins),
-            lambda: finish_extreme(0, 2 * F, maxs),
-            lambda: finish_mean(0),
-            lambda: finish_std(0, 0),
-            lambda: finish_std(0, 1),
+            lambda: finish(0, 0, means),
+            lambda: finish(0, F, mins),
+            lambda: finish(0, 2 * F, maxs),
+            lambda: finish_std(0),
             lambda: store_columns(0, 0, 4 * F),
         ]
         open_rows(0)
@@ -409,42 +347,31 @@ def tile_gnnlayer_pa_t_kernel(tc, x, e_enc, W_pre_words, W_pre_scales, b_pre, ou
                 e_rows[r + LOAD_AHEAD] = load_round(r + LOAD_AHEAD)
             if r + 1 < ROUNDS:
                 turn_round(r + 1)
-            if r == 1:
+            if r == 2:
                 finish_target_term(target)
             if 0 <= r - FINISH_FROM < len(finish_steps):
                 finish_steps[r - FINISH_FROM]()
             if r + 1 < ROUNDS:
                 quantise_round(r + 1)
-            if r == FINISH_FROM:
-                square_the_sums(0)
             open_round(r)
             for h in range(F_HALVES):
                 multiply(r, h)
-                square(r, h)
                 if r < ROUNDS - 1:
                     reduce_all(r, h)
-            halve_squares(r)
 
         last = ROUNDS - 1
-        reduce(last, 0, sums, ALU.add)
-        reduce(last, 0, mins, ALU.min)
-        reduce(last, 0, maxs, ALU.max)
-        reduce(last, 1, sums, ALU.add)
-        last_squares = keep.tile([P, F_HALVES, PAIRS], F32)
-        nc.vector.tensor_reduce(out=last_squares[:], in_=partial_last[:], axis=AXIS_X, op=ALU.add)
-        square_the_sums(1)
-        nc.vector.tensor_tensor(
-            out=minus_square[:, :, last_pairs], in0=minus_square[:, :, last_pairs],
-            in1=last_squares[:], op=ALU.add,
-        )
-        reduce(last, 1, mins, ALU.min)
-        reduce(last, 1, maxs, ALU.max)
+        for h in range(F_HALVES):
+            mean_and_variance(last, h)
+        for h in range(F_HALVES):
+            reduce(last, h, mins, ALU.min)
+            reduce(last, h, maxs, ALU.max)
 
         open_rows(1)
         cols = targets(1)
-        open_groups = [open_std(1, h) for h in range(F_HALVES)]
-        mean_back = open_mean()
-        turn_mean(1, 0, mean_back)
+        finish_std(1)
+        store_columns(1, 3 * F, F)
+        finish(1, 0, means)
+        store_columns(1, 0, F)
         first_back = turned_pool.tile([P, 2, P], F32, tag="turned")
         for a, aggregate in enumerate((mins, maxs)):
             turn_and_add(first_back[:, a, :], [tgt_bias[:, 0, cols], aggregate[:, 0, cols]])
@@ -452,12 +379,6 @@ def tile_gnnlayer_pa_t_kernel(tc, x, e_enc, W_pre_words, W_pre_scales, b_pre, ou
             out=out_rows_of[1][:, F : 3 * F].rearrange("p (a h f) -> p a h f", a=2, h=F_HALVES)[:, :, 0, :],
             in_=first_back[:],
         )
-        turn_mean(1, 1, mean_back)
-        copy_mean(1, mean_back)
-        store_columns(1, 0, F)
-        for h in range(F_HALVES):
-            close_std(1, h, open_groups[h])
-        store_columns(1, 3 * F, F)
         for first, aggregate in ((F, mins), (2 * F, maxs)):
             back = turned_pool.tile([P, P], F32, tag="turned")
             turn_and_add(back[:], [tgt_bias[:, 1, cols], aggregate[:, 1, cols]])

@@ -32,6 +32,7 @@ ROUNDS = N // I_ROUND
 I_STORE = P // B
 ROUNDS_STORE = I_STORE // I_ROUND
 LOAD_AHEAD = 4
+SORTED_TILES = 3
 FINISH_FROM = ROUNDS_STORE + 1
 
 FLOPS = 2 * (B * N * N + 2 * B * N) * C * F
@@ -42,6 +43,7 @@ def tile_gnnlayer_pa_t_kernel(tc, x, e_enc, W_pre_words, W_pre_scales, b_pre, ou
     with ExitStack() as stack:
         keep = stack.enter_context(tc.tile_pool(name="keep", bufs=1))
         rows_pool = stack.enter_context(tc.tile_pool(name="rows", bufs=LOAD_AHEAD * TILES))
+        sorted_pool = stack.enter_context(tc.tile_pool(name="sorted", bufs=2 * SORTED_TILES))
         stage = stack.enter_context(tc.tile_pool(name="stage", bufs=2))
         turned_pool = stack.enter_context(tc.psum_pool(name="turned", bufs=4))
         acc_pool = stack.enter_context(tc.psum_pool(name="acc", bufs=4))
@@ -106,14 +108,21 @@ def tile_gnnlayer_pa_t_kernel(tc, x, e_enc, W_pre_words, W_pre_scales, b_pre, ou
             in_=ident[:].rearrange("p (j b) -> p b j", b=B_TILE),
         )
 
-        def turn_rows(rows, grouped, first_col, copy):
-            words = rows.bitcast(F32)
+        def sort_words(rows):
+            words = sorted_pool.tile([P, PASSES, 2, P], F32)
+            nc.scalar.copy(
+                out=words[:],
+                in_=rows.bitcast(F32).rearrange("r (g p u) -> r g u p", g=PASSES, u=2),
+            )
+            return words[:]
+
+        def turn_rows(rows, grouped, first_col, copy, words=None):
+            if words is None:
+                words = rows.bitcast(F32).rearrange("r (g p u) -> r g u p", g=PASSES, u=2)
             turned = turned_pool.tile([P, PASSES, 2, P], F32)
             for g in range(PASSES):
                 for u in range(2):
-                    nc.tensor.transpose(
-                        turned[:, g, u, :], words[:, 2 * P * g + u : 2 * P * (g + 1) : 2], perm[:]
-                    )
+                    nc.tensor.transpose(turned[:, g, u, :], words[:, g, u, :], perm[:])
             copy(
                 out=grouped[:, :, first_col : first_col + P, :],
                 in_=turned[:].rearrange("p g u r -> p g r u"),
@@ -151,13 +160,18 @@ def tile_gnnlayer_pa_t_kernel(tc, x, e_enc, W_pre_words, W_pre_scales, b_pre, ou
             }
 
         grouped_of = {}
+        sorted_words = {}
         quantised = {}
 
         def turn_round(r):
             grouped = stage.tile([P, PASSES, COLS, 2], F32, align_bytes=64, tag="grouped")
             for t in range(TILES):
-                turn_rows(e_rows[r][t][:], grouped, P * t, nc.scalar.copy)
+                turn_rows(e_rows[r][t][:], grouped, P * t, nc.scalar.copy, sorted_words.get((r, t)))
             grouped_of[r] = grouped
+
+        def sort_round(r):
+            for t in range(SORTED_TILES):
+                sorted_words[r, t] = sort_words(e_rows[r][t][:])
 
         def turn_and_quantise_first_round():
             grouped = stage.tile([P, PASSES, COLS, 2], F32, align_bytes=64, tag="grouped")
@@ -347,6 +361,8 @@ def tile_gnnlayer_pa_t_kernel(tc, x, e_enc, W_pre_words, W_pre_scales, b_pre, ou
                 e_rows[r + LOAD_AHEAD] = load_round(r + LOAD_AHEAD)
             if r + 1 < ROUNDS:
                 turn_round(r + 1)
+            if r + 2 < ROUNDS:
+                sort_round(r + 2)
             if r == 2:
                 finish_target_term(target)
             if 0 <= r - FINISH_FROM < len(finish_steps):

@@ -32,7 +32,8 @@ ROUNDS = N // I_ROUND
 I_STORE = P // B
 ROUNDS_STORE = I_STORE // I_ROUND
 LOAD_AHEAD = 4
-SORTED_TILES = 3
+SIDE = F_HALVES - 1
+SORTED_TILES = 1
 FINISH_FROM = ROUNDS_STORE + 1
 
 FLOPS = 2 * (B * N * N + 2 * B * N) * C * F
@@ -43,6 +44,7 @@ def tile_gnnlayer_pa_t_kernel(tc, x, e_enc, W_pre_words, W_pre_scales, b_pre, ou
     with ExitStack() as stack:
         keep = stack.enter_context(tc.tile_pool(name="keep", bufs=1))
         rows_pool = stack.enter_context(tc.tile_pool(name="rows", bufs=LOAD_AHEAD * TILES))
+        side_pool = stack.enter_context(tc.tile_pool(name="side", bufs=3))
         sorted_pool = stack.enter_context(tc.tile_pool(name="sorted", bufs=2 * SORTED_TILES))
         stage = stack.enter_context(tc.tile_pool(name="stage", bufs=2))
         turned_pool = stack.enter_context(tc.psum_pool(name="turned", bufs=4))
@@ -167,6 +169,8 @@ def tile_gnnlayer_pa_t_kernel(tc, x, e_enc, W_pre_words, W_pre_scales, b_pre, ou
             grouped = stage.tile([P, PASSES, COLS, 2], F32, align_bytes=64, tag="grouped")
             for t in range(TILES):
                 turn_rows(e_rows[r][t][:], grouped, P * t, nc.scalar.copy, sorted_words.get((r, t)))
+            if r - 2 in sides:
+                halve_side(r - 2)
             grouped_of[r] = grouped
 
         def sort_round(r):
@@ -240,17 +244,55 @@ def tile_gnnlayer_pa_t_kernel(tc, x, e_enc, W_pre_words, W_pre_scales, b_pre, ou
             )
 
         def mean_and_variance(r, h):
+            if h == SIDE and r in sides:
+                by_pair = sides[r][0][:]
+            else:
+                by_pair = accs_of[r][h][:].rearrange("p (c j) -> p c j", j=N)
             for c in range(0, PAIRS, 2):
                 pairs = slice(PAIRS * r + c, PAIRS * r + c + 2)
                 nc.vector.bn_stats(
                     out=stats[:, h, pairs, :].rearrange("p c v -> p (c v)"),
-                    in_=accs_of[r][h][:, N * c : N * (c + 2)].rearrange("p (c j) -> p j c", c=2),
+                    in_=by_pair[:, c : c + 2, :].rearrange("p c j -> p j c"),
                 )
 
         def reduce_all(r, h):
             mean_and_variance(r, h)
             reduce(r, h, mins, ALU.min)
             reduce(r, h, maxs, ALU.max)
+
+        sides = {}
+
+        def copy_side(r):
+            side = side_pool.tile([P, PAIRS, N], F32)
+            nc.scalar.copy(
+                out=side[:].rearrange("p c j -> p (c j)"), in_=accs_of[r][SIDE][:]
+            )
+            excess = side_pool.tile([P, PAIRS, N // 2], F32)
+            nc.gpsimd.tensor_tensor(
+                out=excess[:], in0=side[:, :, 0 : N // 2], in1=side[:, :, N // 2 : N],
+                op=ALU.subtract,
+            )
+            sides[r] = (side, excess)
+
+        def halve_side(r):
+            side, excess = sides[r]
+            nc.scalar.activation(out=excess[:], in_=excess[:], func=ACT.Relu)
+            upper = side_pool.tile([P, PAIRS, N // 2], F32)
+            nc.gpsimd.tensor_tensor(
+                out=upper[:], in0=side[:, :, N // 2 : N], in1=excess[:], op=ALU.add
+            )
+            lower = side_pool.tile([P, PAIRS, N // 2], F32)
+            nc.gpsimd.tensor_tensor(
+                out=lower[:], in0=side[:, :, 0 : N // 2], in1=excess[:], op=ALU.subtract
+            )
+            sides[r] = (lower, upper)
+
+        def reduce_side(r):
+            pairs = slice(PAIRS * r, PAIRS * (r + 1))
+            for aggregate, half, op in zip((mins, maxs), sides[r], (ALU.min, ALU.max)):
+                nc.vector.tensor_reduce(
+                    out=aggregate[:, SIDE, pairs], in_=half[:], axis=AXIS_X, op=op
+                )
 
         bias = keep.tile([P, F_HALVES], F32)
         tgt_bias = keep.tile([P, F_HALVES, N * B], F32)
@@ -372,12 +414,18 @@ def tile_gnnlayer_pa_t_kernel(tc, x, e_enc, W_pre_words, W_pre_scales, b_pre, ou
             open_round(r)
             for h in range(F_HALVES):
                 multiply(r, h)
-                if r < ROUNDS - 1:
-                    reduce_all(r, h)
+            if r < ROUNDS - 1:
+                reduce_all(r, 0)
+                copy_side(r)
+                mean_and_variance(r, SIDE)
+            if r - 1 in sides and r < ROUNDS - 1:
+                reduce_side(r - 1)
 
         last = ROUNDS - 1
-        for h in range(F_HALVES):
-            mean_and_variance(last, h)
+        halve_side(last - 1)
+        mean_and_variance(last, 0)
+        reduce_side(last - 1)
+        mean_and_variance(last, 1)
         for h in range(F_HALVES):
             reduce(last, h, mins, ALU.min)
             reduce(last, h, maxs, ALU.max)

@@ -51,6 +51,19 @@ def tile_gnnlayer_pa_t_kernel(tc, x, e_enc, W_pre_words, W_pre_scales, b_pre, ou
         acc_pool = stack.enter_context(tc.psum_pool(name="acc", bufs=4))
         stack.enter_context(tc.manual_schedule())
 
+        zeros = keep.tile([P, F], BF16)
+        nc.vector.memset(zeros[:], 0.0)
+
+        def warm_up(count):
+            acc = acc_pool.tile([P, F], F32, tag="acc")
+            for step in range(count):
+                nc.tensor.matmul(
+                    out=acc[:], lhsT=zeros[:, 0:P], rhs=zeros[:], start=(step == 0),
+                    stop=(step == count - 1),
+                )
+
+        warm_up(7)
+
         def graphs(half):
             return slice(B_TILE * half, B_TILE * (half + 1))
 
@@ -140,11 +153,8 @@ def tile_gnnlayer_pa_t_kernel(tc, x, e_enc, W_pre_words, W_pre_scales, b_pre, ou
         x_codes = keep.tile([P, PASSES, I_ROUND, B * N], U32, align_bytes=64)
         x_scales = keep.tile([P, PASSES, I_ROUND, B * N], U8, align_bytes=64)
 
-        copies = (nc.scalar.copy, nc.vector.tensor_copy)
-
-        def turn_x():
-            for half, copy in enumerate(copies):
-                turn_rows(x_rows[:, half, :], x_grouped, P * half, copy)
+        def turn_x(half, copy):
+            turn_rows(x_rows[:, half, :], x_grouped, P * half, copy)
 
         def quantise_x():
             for g in range(PASSES):
@@ -168,7 +178,9 @@ def tile_gnnlayer_pa_t_kernel(tc, x, e_enc, W_pre_words, W_pre_scales, b_pre, ou
         def turn_round(r):
             grouped = stage.tile([P, PASSES, COLS, 2], F32, align_bytes=64, tag="grouped")
             for t in range(TILES):
-                turn_rows(e_rows[r][t][:], grouped, P * t, nc.scalar.copy, sorted_words.get((r, t)))
+                helped = r in (2, 3) and t == TILES - 1
+                copy = nc.vector.tensor_copy if helped else nc.scalar.copy
+                turn_rows(e_rows[r][t][:], grouped, P * t, copy, sorted_words.get((r, t)))
             if r - 2 in sides:
                 halve_side(r - 2)
             grouped_of[r] = grouped
@@ -183,9 +195,10 @@ def tile_gnnlayer_pa_t_kernel(tc, x, e_enc, W_pre_words, W_pre_scales, b_pre, ou
             scales = stage.tile([P, PASSES, COLS], U8, align_bytes=64, tag="scales")
             for i in range(I_ROUND):
                 cols = slice(B * N * i, B * N * (i + 1))
-                for half, copy in enumerate(copies):
-                    t = B_HALVES * i + half
-                    turn_rows(e_rows[0][t][:], grouped, P * t, copy)
+                for t in range(B_HALVES * i, B_HALVES * (i + 1)):
+                    turn_rows(e_rows[0][t][:], grouped, P * t, nc.scalar.copy)
+                if i > 0:
+                    turn_x(0, nc.vector.tensor_copy)
                 for g in range(PASSES):
                     nc.vector.quantize_mx(
                         out=codes[:, g, cols].bitcast(FP8X4),
@@ -376,9 +389,10 @@ def tile_gnnlayer_pa_t_kernel(tc, x, e_enc, W_pre_words, W_pre_scales, b_pre, ou
             nc.scalar.copy(out=bias[:], in_=bias_turned[:, 0:F_HALVES])
 
         turn_and_quantise_first_round()
-        turn_x()
+        turn_x(1, nc.scalar.copy)
         quantise_x()
         nc.vector.tensor_copy(out=bias_rows32[:], in_=bias_rows[:])
+        warm_up(4)
         open_round(0)
         for add in (add_edges, add_sources):
             for g, h in product(range(PASSES), range(F_HALVES)):
@@ -423,12 +437,13 @@ def tile_gnnlayer_pa_t_kernel(tc, x, e_enc, W_pre_words, W_pre_scales, b_pre, ou
 
         last = ROUNDS - 1
         halve_side(last - 1)
-        mean_and_variance(last, 0)
-        reduce_side(last - 1)
-        mean_and_variance(last, 1)
+        for h in range(F_HALVES):
+            mean_and_variance(last, h)
         for h in range(F_HALVES):
             reduce(last, h, mins, ALU.min)
             reduce(last, h, maxs, ALU.max)
+            if h != SIDE:
+                reduce_side(last - 1)
 
         open_rows(1)
         cols = targets(1)

@@ -30,11 +30,9 @@ COLS = TILES * P
 PAIRS = I_ROUND * B
 ROUNDS = N // I_ROUND
 I_STORE = P // B
-ROUNDS_STORE = I_STORE // I_ROUND
 LOAD_AHEAD = 4
 SIDE = F_HALVES - 1
 SORTED_TILES = 1
-FINISH_FROM = ROUNDS_STORE + 1
 
 FLOPS = 2 * (B * N * N + 2 * B * N) * C * F
 
@@ -404,14 +402,6 @@ def tile_gnnlayer_pa_t_kernel(tc, x, e_enc, W_pre_words, W_pre_scales, b_pre, ou
         quantise_round(1)
         turn_bias()
         target = target_term()
-        finish_steps = [
-            lambda: finish(0, 0, means),
-            lambda: finish(0, F, mins),
-            lambda: finish(0, 2 * F, maxs),
-            lambda: finish_std(0),
-            lambda: store_columns(0, 0, 4 * F),
-        ]
-        open_rows(0)
         for r in range(1, ROUNDS):
             if r + LOAD_AHEAD < ROUNDS:
                 e_rows[r + LOAD_AHEAD] = load_round(r + LOAD_AHEAD)
@@ -421,8 +411,6 @@ def tile_gnnlayer_pa_t_kernel(tc, x, e_enc, W_pre_words, W_pre_scales, b_pre, ou
                 sort_round(r + 2)
             if r == 2:
                 finish_target_term(target)
-            if 0 <= r - FINISH_FROM < len(finish_steps):
-                finish_steps[r - FINISH_FROM]()
             if r + 1 < ROUNDS:
                 quantise_round(r + 1)
             open_round(r)
@@ -445,12 +433,18 @@ def tile_gnnlayer_pa_t_kernel(tc, x, e_enc, W_pre_words, W_pre_scales, b_pre, ou
             if h != SIDE:
                 reduce_side(last - 1)
 
+        open_rows(0)
+        finish(0, 0, means)
+        finish(0, F, mins)
+        finish(0, 2 * F, maxs)
+        finish_std(0)
+        store_columns(0, 0, 4 * F)
         open_rows(1)
-        cols = targets(1)
         finish_std(1)
         store_columns(1, 3 * F, F)
         finish(1, 0, means)
         store_columns(1, 0, F)
+        cols = targets(1)
         first_back = turned_pool.tile([P, 2, P], F32, tag="turned")
         for a, aggregate in enumerate((mins, maxs)):
             turn_and_add(first_back[:, a, :], [tgt_bias[:, 0, cols], aggregate[:, 0, cols]])

@@ -32,7 +32,7 @@ ROUNDS = N // I_ROUND
 I_STORE = P // B
 LOAD_AHEAD = 4
 SIDE = F_HALVES - 1
-SORTED_TILES = 1
+SORTED_TILES = 2
 
 FLOPS = 2 * (B * N * N + 2 * B * N) * C * F
 
@@ -184,7 +184,7 @@ def tile_gnnlayer_pa_t_kernel(tc, x, e_enc, W_pre_words, W_pre_scales, b_pre, ou
             grouped_of[r] = grouped
 
         def sort_round(r):
-            for t in range(SORTED_TILES):
+            for t in range(SORTED_TILES - r % 2):
                 sorted_words[r, t] = sort_words(e_rows[r][t][:])
 
         def turn_and_quantise_first_round():

from contextlib import ExitStack
from itertools import product

import concourse.mybir as mybir
from concourse.masks import make_identity

F32 = mybir.dt.float32
BF16 = mybir.dt.bfloat16
I32 = mybir.dt.int32
U32 = mybir.dt.uint32
U8 = mybir.dt.uint8
FP8X4 = mybir.dt.float8_e4m3fn_x4
FP4X4 = mybir.dt.float4_e2m1fn_x4
ALU = mybir.AluOpType
ACT = mybir.ActivationFunctionType
AXIS_X = mybir.AxisListType.X

B, N, C, F = 8, 32, 1024, 256
EPS_STD = 1e-5
P = 128
K_PASS = 4 * P
PASSES = C // K_PASS
W_TGT, W_SRC, W_EDGE = 0, PASSES, 2 * PASSES
F_HALVES = F // P
B_TILE = P // N
B_HALVES = B // B_TILE
I_ROUND = 2
TILES = I_ROUND * B_HALVES
COLS = TILES * P
PAIRS = I_ROUND * B
ROUNDS = N // I_ROUND
I_STORE = P // B
LOAD_AHEAD = 4
SIDE = F_HALVES - 1
SORTED_TILES = 2

FLOPS = 2 * (B * N * N + 2 * B * N) * C * F


def tile_gnnlayer_pa_t_kernel(tc, x, e_enc, W_pre_words, W_pre_scales, b_pre, out):
    nc = tc.nc
    with ExitStack() as stack:
        keep = stack.enter_context(tc.tile_pool(name="keep", bufs=1))
        rows_pool = stack.enter_context(tc.tile_pool(name="rows", bufs=LOAD_AHEAD * TILES))
        side_pool = stack.enter_context(tc.tile_pool(name="side", bufs=3))
        sorted_pool = stack.enter_context(tc.tile_pool(name="sorted", bufs=2 * SORTED_TILES))
        stage = stack.enter_context(tc.tile_pool(name="stage", bufs=2))
        turned_pool = stack.enter_context(tc.psum_pool(name="turned", bufs=4))
        acc_pool = stack.enter_context(tc.psum_pool(name="acc", bufs=4))
        stack.enter_context(tc.manual_schedule())

        zeros = keep.tile([P, F], BF16)
        nc.vector.memset(zeros[:], 0.0)

        def warm_up(count):
            acc = acc_pool.tile([P, F], F32, tag="acc")
            for step in range(count):
                nc.tensor.matmul(
                    out=acc[:], lhsT=zeros[:, 0:P], rhs=zeros[:], start=(step == 0),
                    stop=(step == count - 1),
                )

        warm_up(7)

        def graphs(half):
            return slice(B_TILE * half, B_TILE * (half + 1))

        def load_rows(rows, source):
            nc.sync.dma_start(out=rows[:], in_=source.rearrange("b j k -> j b k"))

        def load_round(r):
            tiles = []
            for i in range(I_ROUND):
                for half in range(B_HALVES):
                    e_tile = rows_pool.tile([P, C], BF16)
                    load_rows(e_tile, e_enc[graphs(half), I_ROUND * r + i])
                    tiles.append(e_tile)
            return tiles

        e_rows = {0: load_round(0)}
        x_rows = keep.tile([P, B_HALVES, C], BF16)
        for half in range(B_HALVES):
            load_rows(x_rows[:, half, :], x[graphs(half)])
        w_scales = keep.tile([P, 3 * PASSES, F], U8, align_bytes=64)
        nc.vector.memset(w_scales[:].bitcast(I32), 0)
        for quadrant in range(4):
            nc.sync.dma_start(
                out=w_scales[32 * quadrant : 32 * quadrant + 4].bitcast(I32),
                in_=W_pre_scales.bitcast(I32)[:, 4 * quadrant : 4 * quadrant + 4, :].rearrange(
                    "g s n -> s g n"
                ),
            )
        w_words = keep.tile([P, 3 * PASSES, 2 * F], U8, align_bytes=64)

        def load_words(first, end):
            nc.sync.dma_start(
                out=w_words[:, first:end].bitcast(I32),
                in_=W_pre_words.bitcast(I32)[first:end].rearrange("g p n -> p g n"),
            )

        load_words(W_SRC, 3 * PASSES)
        bias_rows = keep.tile([P, P], BF16)
        nc.vector.memset(bias_rows[:], 0.0)
        nc.sync.dma_start(
            out=bias_rows[0:F_HALVES, :], in_=b_pre.rearrange("(h f) -> h f", h=F_HALVES)
        )
        e_rows[1] = load_round(1)
        load_words(W_TGT, W_SRC)
        for r in range(2, LOAD_AHEAD):
            e_rows[r] = load_round(r)

        one = keep.tile([P, 1], F32)
        nc.vector.memset(one[:], 1.0)
        nc.scalar.activation(out=one[:], in_=one[:], func=ACT.Sqrt)

        ident = keep.tile([P, P], F32)
        make_identity(nc, ident[:])
        perm = keep.tile([P, P], F32)
        nc.vector.tensor_copy(
            out=perm[:].rearrange("p (b j) -> p b j", b=B_TILE),
            in_=ident[:].rearrange("p (j b) -> p b j", b=B_TILE),
        )

        def sort_words(rows):
            words = sorted_pool.tile([P, PASSES, 2, P], F32)
            nc.scalar.copy(
                out=words[:],
                in_=rows.bitcast(F32).rearrange("r (g p u) -> r g u p", g=PASSES, u=2),
            )
            return words[:]

        def turn_rows(rows, grouped, first_col, copy, words=None):
            if words is None:
                words = rows.bitcast(F32).rearrange("r (g p u) -> r g u p", g=PASSES, u=2)
            turned = turned_pool.tile([P, PASSES, 2, P], F32)
            for g in range(PASSES):
                for u in range(2):
                    nc.tensor.transpose(turned[:, g, u, :], words[:, g, u, :], perm[:])
            copy(
                out=grouped[:, :, first_col : first_col + P, :],
                in_=turned[:].rearrange("p g u r -> p g r u"),
            )

        def weight(g, h):
            return {
                "lhsT": w_words[:, g, 2 * P * h : 2 * P * (h + 1)].bitcast(FP4X4),
                "lhsT_scale": w_scales[:, g, P * h : P * (h + 1)],
            }

        x_grouped = keep.tile([P, PASSES, B * N, 2], F32, align_bytes=64)
        x_codes = keep.tile([P, PASSES, I_ROUND, B * N], U32, align_bytes=64)
        x_scales = keep.tile([P, PASSES, I_ROUND, B * N], U8, align_bytes=64)

        def turn_x(half, copy):
            turn_rows(x_rows[:, half, :], x_grouped, P * half, copy)

        def quantise_x():
            for g in range(PASSES):
                for i in range(I_ROUND):
                    nc.vector.quantize_mx(
                        out=x_codes[:, g, i, :].bitcast(FP8X4),
                        scales=x_scales[:, g, i, :],
                        in_=x_grouped[:, g].rearrange("p c u -> p (c u)").bitcast(BF16),
                    )

        def x_operand(g):
            return {
                "rhs": x_codes[:, g].rearrange("p i c -> p (i c)").bitcast(FP8X4),
                "rhs_scale": x_scales[:, g].rearrange("p i c -> p (i c)"),
            }

        grouped_of = {}
        sorted_words = {}
        quantised = {}

        def turn_round(r):
            grouped = stage.tile([P, PASSES, COLS, 2], F32, align_bytes=64, tag="grouped")
            for t in range(TILES):
                helped = r in (2, 3) and t == TILES - 1
                copy = nc.vector.tensor_copy if helped else nc.scalar.copy
                turn_rows(e_rows[r][t][:], grouped, P * t, copy, sorted_words.get((r, t)))
            if r - 2 in sides:
                halve_side(r - 2)
            grouped_of[r] = grouped

        def sort_round(r):
            for t in range(SORTED_TILES - r % 2):
                sorted_words[r, t] = sort_words(e_rows[r][t][:])

        def turn_and_quantise_first_round():
            grouped = stage.tile([P, PASSES, COLS, 2], F32, align_bytes=64, tag="grouped")
            codes = stage.tile([P, PASSES, COLS], U32, align_bytes=64, tag="codes")
            scales = stage.tile([P, PASSES, COLS], U8, align_bytes=64, tag="scales")
            for i in range(I_ROUND):
                cols = slice(B * N * i, B * N * (i + 1))
                for t in range(B_HALVES * i, B_HALVES * (i + 1)):
                    turn_rows(e_rows[0][t][:], grouped, P * t, nc.scalar.copy)
                if i > 0:
                    turn_x(0, nc.vector.tensor_copy)
                for g in range(PASSES):
                    nc.vector.quantize_mx(
                        out=codes[:, g, cols].bitcast(FP8X4),
                        scales=scales[:, g, cols],
                        in_=grouped[:, g, cols, :].rearrange("p c u -> p (c u)").bitcast(BF16),
                    )
            quantised[0] = (codes, scales)

        def quantise_round(r):
            codes = stage.tile([P, PASSES, COLS], U32, align_bytes=64, tag="codes")
            scales = stage.tile([P, PASSES, COLS], U8, align_bytes=64, tag="scales")
            nc.vector.quantize_mx(
                out=codes[:].rearrange("p g c -> p (g c)").bitcast(FP8X4),
                scales=scales[:].rearrange("p g c -> p (g c)"),
                in_=grouped_of[r][:].rearrange("p g c u -> p (g c u)").bitcast(BF16),
            )
            quantised[r] = (codes, scales)

        stats = keep.tile([P, F_HALVES, N * B, 3], F32)
        means = stats[:, :, :, 1]
        variances_n = stats[:, :, :, 2]
        mins = keep.tile([P, F_HALVES, N * B], F32)
        maxs = keep.tile([P, F_HALVES, N * B], F32)

        accs_of = {}

        def open_round(r):
            accs = []
            for h in range(F_HALVES):
                acc = acc_pool.tile([P, COLS], F32, tag="acc")
                accs.append(acc)
            accs_of[r] = accs

        def add_edges(r, h, g):
            codes, scales = quantised[r]
            nc.tensor.matmul_mx(
                out=accs_of[r][h][:], start=(g == 0), stop=False, **weight(W_EDGE + g, h),
                rhs=codes[:, g, :].bitcast(FP8X4), rhs_scale=scales[:, g, :],
            )

        def add_sources(r, h, g):
            nc.tensor.matmul_mx(
                out=accs_of[r][h][:], start=False, stop=(g == PASSES - 1),
                **weight(W_SRC + g, h), **x_operand(g),
            )

        def multiply(r, h):
            for add in (add_edges, add_sources):
                for g in range(PASSES):
                    add(r, h, g)

        def reduce(r, h, aggregate, op):
            nc.vector.tensor_reduce(
                out=aggregate[:, h, PAIRS * r : PAIRS * (r + 1)],
                in_=accs_of[r][h][:].rearrange("p (c j) -> p c j", j=N), axis=AXIS_X, op=op,
            )

        def mean_and_variance(r, h):
            if h == SIDE and r in sides:
                by_pair = sides[r][0][:]
            else:
                by_pair = accs_of[r][h][:].rearrange("p (c j) -> p c j", j=N)
            for c in range(0, PAIRS, 2):
                pairs = slice(PAIRS * r + c, PAIRS * r + c + 2)
                nc.vector.bn_stats(
                    out=stats[:, h, pairs, :].rearrange("p c v -> p (c v)"),
                    in_=by_pair[:, c : c + 2, :].rearrange("p c j -> p j c"),
                )

        def reduce_all(r, h):
            mean_and_variance(r, h)
            reduce(r, h, mins, ALU.min)
            reduce(r, h, maxs, ALU.max)

        sides = {}

        def copy_side(r):
            side = side_pool.tile([P, PAIRS, N], F32)
            nc.scalar.copy(
                out=side[:].rearrange("p c j -> p (c j)"), in_=accs_of[r][SIDE][:]
            )
            excess = side_pool.tile([P, PAIRS, N // 2], F32)
            nc.gpsimd.tensor_tensor(
                out=excess[:], in0=side[:, :, 0 : N // 2], in1=side[:, :, N // 2 : N],
                op=ALU.subtract,
            )
            sides[r] = (side, excess)

        def halve_side(r):
            side, excess = sides[r]
            nc.scalar.activation(out=excess[:], in_=excess[:], func=ACT.Relu)
            upper = side_pool.tile([P, PAIRS, N // 2], F32)
            nc.gpsimd.tensor_tensor(
                out=upper[:], in0=side[:, :, N // 2 : N], in1=excess[:], op=ALU.add
            )
            lower = side_pool.tile([P, PAIRS, N // 2], F32)
            nc.gpsimd.tensor_tensor(
                out=lower[:], in0=side[:, :, 0 : N // 2], in1=excess[:], op=ALU.subtract
            )
            sides[r] = (lower, upper)

        def reduce_side(r):
            pairs = slice(PAIRS * r, PAIRS * (r + 1))
            for aggregate, half, op in zip((mins, maxs), sides[r], (ALU.min, ALU.max)):
                nc.vector.tensor_reduce(
                    out=aggregate[:, SIDE, pairs], in_=half[:], axis=AXIS_X, op=op
                )

        bias = keep.tile([P, F_HALVES], F32)
        tgt_bias = keep.tile([P, F_HALVES, N * B], F32)
        out_by_i = out.rearrange("b i c -> i b c")
        out_rows_of = {}
        eps = keep.tile([P, 1], F32)
        nc.vector.memset(eps[:], EPS_STD)

        def targets(store):
            return slice(P * store, P * (store + 1))

        def turn_and_add(back, terms):
            for t, term in enumerate(terms):
                nc.tensor.matmul(
                    out=back, lhsT=term, rhs=ident[:], is_transpose=True,
                    start=(t == 0), stop=(t == len(terms) - 1),
                )

        def store_columns(store, first, width):
            nc.sync.dma_start(
                out=out_by_i[I_STORE * store : I_STORE * (store + 1), :, first : first + width],
                in_=out_rows_of[store][:, first : first + width],
            )

        def open_rows(store):
            out_rows = stage.tile([P, 4 * F], F32)
            out_rows_of[store] = out_rows

        def finish(store, first, aggregate):
            cols = targets(store)
            back = turned_pool.tile([P, F_HALVES, P], F32, tag="turned")
            for h in range(F_HALVES):
                turn_and_add(back[:, h, :], [tgt_bias[:, h, cols], aggregate[:, h, cols]])
            nc.scalar.copy(
                out=out_rows_of[store][:, first : first + F],
                in_=back[:].rearrange("p h f -> p (h f)"),
            )

        variance = keep.tile([P, F], F32)

        def finish_std(store):
            back = turned_pool.tile([P, F_HALVES, P], F32, tag="turned")
            for h in range(F_HALVES):
                turn_and_add(back[:, h, :], [variances_n[:, h, targets(store)]])
            nc.scalar.activation(
                out=variance[:], in_=back[:].rearrange("p h f -> p (h f)"), func=ACT.Relu,
                scale=1.0 / N,
            )
            nc.scalar.activation(
                out=out_rows_of[store][:, 3 * F : 4 * F], in_=variance[:], func=ACT.Sqrt,
                bias=eps[:],
            )

        def target_term():
            acc = acc_pool.tile([P, F_HALVES, B * N], F32, tag="acc")
            for h in range(F_HALVES):
                for half in range(B_HALVES):
                    cols = slice(P * half, P * (half + 1))
                    for g in range(PASSES):
                        nc.tensor.matmul_mx(
                            out=acc[:, h, cols], start=(g == 0), stop=(g == PASSES - 1),
                            **weight(W_TGT + g, h), rhs=x_codes[:, g, 0, cols].bitcast(FP8X4),
                            rhs_scale=x_scales[:, g, 0, cols],
                        )
            return acc

        def finish_target_term(acc):
            for h in range(F_HALVES):
                nc.scalar.activation(
                    out=tgt_bias[:, h].rearrange("p (i b) -> p i b", b=B),
                    in_=acc[:, h].rearrange("p (b i) -> p i b", b=B),
                    func=ACT.Identity,
                    bias=bias[:, h : h + 1],
                )

        bias_rows32 = keep.tile([P, P], F32)

        def turn_bias():
            bias_turned = turned_pool.tile([P, P], F32, tag="turned")
            nc.tensor.transpose(bias_turned[:], bias_rows32[:], ident[:])
            nc.scalar.copy(out=bias[:], in_=bias_turned[:, 0:F_HALVES])

        turn_and_quantise_first_round()
        turn_x(1, nc.scalar.copy)
        quantise_x()
        nc.vector.tensor_copy(out=bias_rows32[:], in_=bias_rows[:])
        warm_up(4)
        open_round(0)
        for add in (add_edges, add_sources):
            for g, h in product(range(PASSES), range(F_HALVES)):
                add(0, h, g)
        for h in range(F_HALVES):
            reduce_all(0, h)
        e_rows[LOAD_AHEAD] = load_round(LOAD_AHEAD)
        turn_round(1)
        quantise_round(1)
        turn_bias()
        target = target_term()
        for r in range(1, ROUNDS):
            if r + LOAD_AHEAD < ROUNDS:
                e_rows[r + LOAD_AHEAD] = load_round(r + LOAD_AHEAD)
            if r + 1 < ROUNDS:
                turn_round(r + 1)
            if r + 2 < ROUNDS:
                sort_round(r + 2)
            if r == 2:
                finish_target_term(target)
            if r + 1 < ROUNDS:
                quantise_round(r + 1)
            open_round(r)
            for h in range(F_HALVES):
                multiply(r, h)
            if r < ROUNDS - 1:
                reduce_all(r, 0)
                copy_side(r)
                mean_and_variance(r, SIDE)
            if r - 1 in sides and r < ROUNDS - 1:
                reduce_side(r - 1)

        last = ROUNDS - 1
        halve_side(last - 1)
        for h in range(F_HALVES):
            mean_and_variance(last, h)
        for h in range(F_HALVES):
            reduce(last, h, mins, ALU.min)
            reduce(last, h, maxs, ALU.max)
            if h != SIDE:
                reduce_side(last - 1)

        open_rows(0)
        finish(0, 0, means)
        finish(0, F, mins)
        finish(0, 2 * F, maxs)
        finish_std(0)
        store_columns(0, 0, 4 * F)
        open_rows(1)
        finish_std(1)
        store_columns(1, 3 * F, F)
        finish(1, 0, means)
        store_columns(1, 0, F)
        cols = targets(1)
        first_back = turned_pool.tile([P, 2, P], F32, tag="turned")
        for a, aggregate in enumerate((mins, maxs)):
            turn_and_add(first_back[:, a, :], [tgt_bias[:, 0, cols], aggregate[:, 0, cols]])
        nc.scalar.copy(
            out=out_rows_of[1][:, F : 3 * F].rearrange("p (a h f) -> p a h f", a=2, h=F_HALVES)[:, :, 0, :],
            in_=first_back[:],
        )
        for first, aggregate in ((F, mins), (2 * F, maxs)):
            back = turned_pool.tile([P, P], F32, tag="turned")
            turn_and_add(back[:], [tgt_bias[:, 1, cols], aggregate[:, 1, cols]])
            nc.scalar.copy(out=out_rows_of[1][:, first + P : first + F], in_=back[:])
            store_columns(1, first, F)
